import numpy as np
import ml_dtypes


def mxq(x, axis, fmt="e4m3"):
    dtype, down = {"e4m3": (ml_dtypes.float8_e4m3fn, 7), "e5m2": (ml_dtypes.float8_e5m2, 14)}[fmt]
    v = np.moveaxis(np.asarray(x, np.float32).astype(ml_dtypes.bfloat16).astype(np.float64), axis, -1)
    blocks = v.reshape(v.shape[:-1] + (-1, 32))
    amax = np.abs(blocks).max(-1, keepdims=True)
    byte = np.maximum(np.where(amax > 0, np.frexp(amax)[1] - 1 + 127, 0) - down, 1)
    scale = np.exp2(byte - 127.0)
    codes = (blocks / scale).astype(np.float32).astype(dtype).astype(np.float64)
    return np.moveaxis((codes * scale).reshape(v.shape), -1, axis)


WIDE = False


def mx_kscale(k):
    if not WIDE:
        return np.ones(k)
    levels = np.array([10, -10, 5, -5, 0])
    a = np.random.permutation(np.resize(levels, k // 512 * 4)).reshape(k // 512, 4)
    idx = np.arange(k)
    return np.exp2(a[idx // 512, idx % 128 // 32])


BF16 = ml_dtypes.bfloat16


def bf(x):
    return np.asarray(x, np.float32).astype(BF16)


def f64(x):
    return np.asarray(x).astype(np.float64)


E2M1 = np.array([0.0, 0.5, 1.0, 1.5, 2.0, 3.0, 4.0, 6.0, -0.0, -0.5, -1.0, -1.5, -2.0, -3.0, -4.0, -6.0])


def pack_weight(w, fmt):
    k, n = w.shape
    w = f64(bf(w)).reshape(k // 32, 32, n)
    amax = np.abs(w).max(1)
    if fmt == "e4m3":
        byte = np.frexp(amax)[1] - 1 + 127 - 7
    else:
        mant, ex = np.frexp(amax / 6.0)
        byte = np.where(mant > 0.5, ex, ex - 1) + 127
    byte = np.clip(np.where(amax > 0, byte, 1), 1, 254)
    scaled = (w * np.exp2(127.0 - byte)[:, None, :]).reshape(k, n).astype(np.float32)
    by_word = np.ascontiguousarray(scaled.reshape(k // 512, 128, 4, n).transpose(0, 1, 3, 2))
    if fmt == "e4m3":
        words = by_word.astype(ml_dtypes.float8_e4m3fn).view(np.uint8)
    else:
        c = by_word.astype(ml_dtypes.float4_e2m1fn).view(np.uint8) & 0xF
        words = c[..., 0::2] | (c[..., 1::2] << 4)
    return np.ascontiguousarray(words), np.ascontiguousarray(byte.astype(np.uint8).reshape(k // 512, 16, n))


def unpack_weight(words, scales, fmt):
    g, p, n, _ = words.shape
    if fmt == "e4m3":
        vals = np.ascontiguousarray(words).view(ml_dtypes.float8_e4m3fn).astype(np.float64)
    else:
        nib = np.empty((g, p, n, 4), np.uint8)
        nib[..., 0::2] = words & 0xF
        nib[..., 1::2] = words >> 4
        vals = E2M1[nib]
    vals = vals * np.repeat(np.exp2(scales.astype(np.float64) - 127.0), 8, axis=1)[..., None]
    return vals.transpose(0, 1, 3, 2).reshape(g * 512, n)


B, IN, H, OUT, L, STEPS = 4096, 512, 512, 128, 3, 3
LN_EPS = 1e-5
TAU_EPS = 1e-6
FMT = "e4m3"


def layer_norm(v, g, b):
    m = v.mean(-1, keepdims=True)
    var = ((v - m) ** 2).mean(-1, keepdims=True)
    return (v - m) / np.sqrt(var + LN_EPS) * g + b


def setup_inputs():
    r = mx_kscale(IN)
    s = mx_kscale(H)
    s = s / s.max()
    t = mx_kscale(H)
    liq_rms = np.sqrt(L * (L + 1) / 2.0)
    liq = bf(np.random.standard_normal((B, H)) * liq_rms * s)
    h = bf(np.random.standard_normal((B, H)))
    x = bf(np.random.standard_normal((B, IN)) * r)
    W_in_words, W_in_scales = pack_weight(np.ascontiguousarray((np.random.standard_normal((H, IN)) * 0.7 / np.sqrt(IN) / r).T), FMT)
    b_in = bf(np.random.standard_normal(H) * 0.3)
    W_v_words, W_v_scales = pack_weight(np.ascontiguousarray((np.random.standard_normal((H, H)) / np.sqrt(H) * t[:, None] / s).T), FMT)
    b_v = bf(np.random.standard_normal(H) * 0.5 * t)
    W_o_words, W_o_scales = pack_weight(np.ascontiguousarray((np.random.standard_normal((H, H)) / np.sqrt(H) / t).T), FMT)
    b_o = bf(np.random.standard_normal(H) * 0.5)
    g_att = bf(1.0 + 0.1 * np.random.standard_normal(H))
    beta_att = bf(np.random.standard_normal(H) * 0.3)
    tau = bf(0.5 + 0.5 * np.random.random(H))
    return {"liq": liq,
            "h": h,
            "x": x,
            "W_in_words": W_in_words,
            "W_in_scales": W_in_scales,
            "b_in": b_in,
            "W_v_words": W_v_words,
            "W_v_scales": W_v_scales,
            "b_v": b_v,
            "W_o_words": W_o_words,
            "W_o_scales": W_o_scales,
            "b_o": b_o,
            "g_att": g_att,
            "beta_att": beta_att,
            "tau": tau}


def reference(liq, h, x, W_in_words, W_in_scales, b_in, W_v_words, W_v_scales, b_v, W_o_words, W_o_scales, b_o, g_att, beta_att, tau):
    liq, h = f64(liq), f64(h)
    xin = (mxq(f64(x), 1, "e4m3") @ unpack_weight(W_in_words, W_in_scales, FMT)) + f64(b_in)
    v = (mxq(liq, 1, "e4m3") @ unpack_weight(W_v_words, W_v_scales, FMT)) + f64(b_v)
    att = (mxq(v, 1, "e4m3") @ unpack_weight(W_o_words, W_o_scales, FMT)) + f64(b_o)
    z = layer_norm(att + liq, f64(g_att), f64(beta_att))
    dh = (-h + np.tanh(z + xin)) / (f64(tau) + TAU_EPS)
    return h + dh

@@ -1,0 +1,430 @@
+from contextlib import ExitStack
+
+import concourse.mybir as mybir
+from concourse.masks import make_identity
+
+F32 = mybir.dt.float32
+BF16 = mybir.dt.bfloat16
+I32 = mybir.dt.int32
+U32 = mybir.dt.uint32
+U8 = mybir.dt.uint8
+FP8X4 = mybir.dt.float8_e4m3fn_x4
+ALU = mybir.AluOpType
+ACT = mybir.ActivationFunctionType
+
+P = 128
+PACK = 4
+ROWS = 4096
+FEAT = 512
+ROW_TILES = ROWS // P
+TILES_PER_CHUNK = 4
+CHUNK_ROWS = TILES_PER_CHUNK * P
+CHUNKS = ROW_TILES // TILES_PER_CHUNK
+SLICES = FEAT // P
+LN_EPS = 1e-5
+TAU_EPS = 1e-6
+W_IN, W_V, W_O = 0, 1, 2
+LIQ, X = 0, 1
+
+LAG_QUANT = 1
+LAG_VALUE = LAG_QUANT + 1
+LAG_NORM = LAG_VALUE + 1
+LAG_SCALE = LAG_NORM + 1
+LAG_DRIVE = LAG_QUANT + TILES_PER_CHUNK + 1
+LAG_GATE = LAG_SCALE + TILES_PER_CHUNK
+LAG_UPDATE = LAG_GATE + SLICES
+LAG_KEEP = LAG_UPDATE - TILES_PER_CHUNK
+LOAD_AHEAD = 5
+
+FLOPS = 3 * 2 * ROWS * FEAT * FEAT
+
+
+def tile_advancedliquidneuralnetwork_pb_t_kernel(
+    tc,
+    liq,
+    h,
+    x,
+    W_in_words,
+    W_in_scales,
+    b_in,
+    W_v_words,
+    W_v_scales,
+    b_v,
+    W_o_words,
+    W_o_scales,
+    b_o,
+    g_att,
+    beta_att,
+    tau,
+    out,
+):
+    nc = tc.nc
+
+    liq_rows = liq.rearrange("(p i) f -> p i f", i=ROW_TILES)
+    h_rows = h.rearrange("(p i) f -> p i f", i=ROW_TILES)
+    x_rows = x.rearrange("(p i) f -> p i f", i=ROW_TILES)
+    out_rows = out.rearrange("(p i) f -> p i f", i=ROW_TILES)
+
+    with ExitStack() as stack:
+        stack.enter_context(tc.manual_schedule())
+        const = stack.enter_context(tc.tile_pool(name="const", bufs=1))
+        loads = stack.enter_context(tc.tile_pool(name="loads", bufs=3))
+        work = stack.enter_context(tc.tile_pool(name="work", bufs=3))
+        psum = stack.enter_context(tc.psum_pool(name="psum", bufs=1))
+
+        live = {}
+
+        def chunk_rows(c):
+            return slice(c * TILES_PER_CHUNK, (c + 1) * TILES_PER_CHUNK)
+
+        def load_chunk(name, rows, c):
+            if c < CHUNKS:
+                live[name, c] = loads.tile([P, TILES_PER_CHUNK, FEAT], BF16, tag=name, name=name, bufs=4 if name == "h" else 3)
+                nc.sync.dma_start(out=live[name, c][:], in_=rows[:, chunk_rows(c), :])
+
+        w_codes = const.tile([P, 3, FEAT], U32, align_bytes=64)
+        w_scales = const.tile([P, 3, FEAT], U8, align_bytes=64)
+        nc.vector.memset(w_scales[:].bitcast(I32), 0)
+        given = {W_V: (W_v_words, W_v_scales), W_O: (W_o_words, W_o_scales), W_IN: (W_in_words, W_in_scales)}
+        for w in (W_V, W_O, W_IN):
+            scale_rows = given[w][1].rearrange("g q n -> (g q) n").bitcast(I32)
+            for quadrant in range(4):
+                nc.sync.dma_start(
+                    out=w_scales[32 * quadrant : 32 * quadrant + 4, w, :].bitcast(I32),
+                    in_=scale_rows[4 * quadrant : 4 * quadrant + 4, :],
+                )
+
+        def load_weight_words(w):
+            nc.sync.dma_start(
+                out=w_codes[:, w, :].bitcast(I32),
+                in_=given[w][0].rearrange("g p n t -> (g p) (n t)").bitcast(I32),
+            )
+
+        load_chunk("liq", liq_rows, 0)
+        load_chunk("x", x_rows, 0)
+        load_weight_words(W_V)
+        load_weight_words(W_O)
+        load_weight_words(W_IN)
+        load_chunk("liq", liq_rows, 1)
+        load_chunk("x", x_rows, 1)
+        load_chunk("h", h_rows, 0)
+
+        ident = const.tile([P, P], F32)
+        make_identity(nc, ident[:])
+        ident_bf = const.tile([P, P], BF16)
+        make_identity(nc, ident_bf[:])
+
+        vec_rows = const.tile([P, P], BF16)
+        nc.vector.memset(vec_rows[:], 0.0)
+        for i, vec in enumerate((b_in, beta_att, g_att, tau)):
+            nc.scalar.dma_start(
+                out=vec_rows[SLICES * i : SLICES * (i + 1), :], in_=vec.rearrange("(m p) -> m p", p=P)
+            )
+        bv_words = const.tile([P, PACK], BF16)
+        nc.scalar.dma_start(out=bv_words[:], in_=b_v.rearrange("(p t) -> p t", t=PACK))
+        bo_rows = const.tile([P, FEAT], BF16)
+        nc.scalar.dma_start(out=bo_rows[:], in_=b_o.partition_broadcast(P))
+        tau_rows = const.tile([P, FEAT], BF16)
+        nc.scalar.dma_start(out=tau_rows[:], in_=tau.partition_broadcast(P))
+
+        vec_ps = psum.tile([P, P], BF16, tag="words")
+        nc.tensor.transpose(vec_ps[:], vec_rows[:], ident_bf[:])
+        vec_cols = const.tile([P, 4 * SLICES], F32)
+        nc.vector.tensor_copy(out=vec_cols[:], in_=vec_ps[:, 0 : 4 * SLICES])
+        shift_col = const.tile([P, SLICES], F32)
+        nc.vector.tensor_add(out=shift_col[:], in0=vec_cols[:, 0:SLICES], in1=vec_cols[:, SLICES : 2 * SLICES])
+        gain_col = vec_cols[:, 2 * SLICES : 3 * SLICES]
+        rate_col = const.tile([P, SLICES], F32)
+        nc.vector.tensor_scalar_add(out=rate_col[:], in0=vec_cols[:, 3 * SLICES : 4 * SLICES], scalar1=TAU_EPS)
+        nc.vector.reciprocal(out=rate_col[:], in_=rate_col[:])
+        keep_rows = const.tile([P, FEAT], F32)
+        nc.vector.tensor_scalar_add(out=keep_rows[:], in0=tau_rows[:], scalar1=TAU_EPS)
+        nc.vector.reciprocal(out=keep_rows[:], in_=keep_rows[:])
+        nc.vector.tensor_scalar(
+            out=keep_rows[:], in0=keep_rows[:], scalar1=-1.0, scalar2=1.0, op0=ALU.mult, op1=ALU.add
+        )
+        minus_half = const.tile([P, 1], F32)
+        nc.vector.memset(minus_half[:], -0.5)
+
+        def in_range(t):
+            return 0 <= t < ROW_TILES
+
+        def mx_rows(acc, codes, scales, w):
+            nc.tensor.matmul_mx(
+                out=acc[:],
+                lhsT=codes.bitcast(FP8X4),
+                lhsT_scale=scales,
+                rhs=w_codes[:, w, :].bitcast(FP8X4),
+                rhs_scale=w_scales[:, w, :],
+                start=True,
+                stop=True,
+            )
+
+        def entry_transposes(t):
+            if in_range(t):
+                c, i = divmod(t, TILES_PER_CHUNK)
+                planes = psum.tile([P, 2, 2, P], F32, tag="words")
+                for s, name in ((LIQ, "liq"), (X, "x")):
+                    words = live[name, c][:, i, :].bitcast(F32)
+                    for u in range(2):
+                        nc.tensor.transpose(planes[:, s, u, :], words[:, u::2], ident[:])
+                live["planes", t] = planes
+
+        def entry_copy(t):
+            if in_range(t):
+                grouped = work.tile([P, 2, P, PACK], BF16, tag="in_grouped", align_bytes=64)
+                grouped_words = (
+                    grouped[:].rearrange("p s r t -> p (s r t)").bitcast(F32).rearrange("p (s r u) -> p s r u", r=P, u=2)
+                )
+                nc.scalar.copy(out=grouped_words, in_=live["planes", t][:].rearrange("p s u r -> p s r u"))
+                live["in_grouped", t] = grouped
+
+        def entry_quantise(t):
+            if in_range(t):
+                c, i = divmod(t, TILES_PER_CHUNK)
+                grouped = live["in_grouped", t]
+                liq_codes = work.tile([P, P], U32, tag="liq_codes", align_bytes=64)
+                liq_scales = work.tile([P, P], U8, tag="liq_scales", align_bytes=64)
+                nc.vector.quantize_mx(
+                    out=liq_codes[:].bitcast(FP8X4),
+                    scales=liq_scales[:],
+                    in_=grouped[:, LIQ, :, :].rearrange("p r t -> p (r t)"),
+                )
+                live["liq_mx", t] = (liq_codes, liq_scales)
+                if i == 0:
+                    x_codes = work.tile([P, CHUNK_ROWS], U32, tag="x_codes", align_bytes=64)
+                    x_scales = work.tile([P, CHUNK_ROWS], U8, tag="x_scales", align_bytes=64)
+                    live["x_mx", c] = (x_codes, x_scales)
+                x_codes, x_scales = live["x_mx", c]
+                nc.vector.quantize_mx(
+                    out=x_codes[:, i * P : (i + 1) * P].bitcast(FP8X4),
+                    scales=x_scales[:, i * P : (i + 1) * P],
+                    in_=grouped[:, X, :, :].rearrange("p r t -> p (r t)"),
+                )
+
+        def value_matmul(t):
+            if in_range(t):
+                liq_codes, liq_scales = live["liq_mx", t]
+                v_ps = psum.tile([P, FEAT], F32, tag="v")
+                mx_rows(v_ps, liq_codes[:], liq_scales[:], W_V)
+                live["v_ps", t] = v_ps
+
+        def value_copy(t):
+            if in_range(t):
+                v_planes = work.tile([P, PACK, P], F32, tag="v_planes")
+                nc.scalar.copy(out=v_planes[:], in_=live["v_ps", t][:].rearrange("r (p t) -> r t p", t=PACK))
+                live["v_planes", t] = v_planes
+
+        def value_transposes(t):
+            if in_range(t):
+                v_planes = live["v_planes", t]
+                vt_ps = psum.tile([P, PACK, P], F32, tag="vt")
+                for j in range(PACK):
+                    nc.tensor.transpose(vt_ps[:, j, :], v_planes[:, j, :], ident[:])
+                live["vt_ps", t] = vt_ps
+
+        def value_quantise(t):
+            if in_range(t):
+                grouped = work.tile([P, P, PACK], BF16, tag="v_grouped", align_bytes=64)
+                nc.vector.tensor_tensor(
+                    out=grouped[:],
+                    in0=live["vt_ps", t][:].rearrange("p t r -> p r t"),
+                    in1=bv_words[:].unsqueeze(1).to_broadcast([P, P, PACK]),
+                    op=ALU.add,
+                )
+                v_codes = work.tile([P, P], U32, tag="v_codes", align_bytes=64)
+                v_scales = work.tile([P, P], U8, tag="v_scales", align_bytes=64)
+                nc.vector.quantize_mx(
+                    out=v_codes[:].bitcast(FP8X4), scales=v_scales[:], in_=grouped[:].rearrange("p r t -> p (r t)")
+                )
+                live["v_mx", t] = (v_codes, v_scales)
+
+        def residual(t):
+            if in_range(t):
+                c, i = divmod(t, TILES_PER_CHUNK)
+                if i == 0:
+                    live["u", c] = work.tile([P, TILES_PER_CHUNK, FEAT], F32, tag="u", name="u")
+                nc.gpsimd.tensor_tensor(out=live["u", c][:, i, :], in0=live["liq", c][:, i, :], in1=bo_rows[:], op=ALU.add)
+
+        def norm_matmul(t):
+            if in_range(t):
+                v_codes, v_scales = live["v_mx", t]
+                att_ps = psum.tile([P, FEAT], F32, tag="att")
+                mx_rows(att_ps, v_codes[:], v_scales[:], W_O)
+                live["att_ps", t] = att_ps
+
+        def norm_mean(t):
+            if in_range(t):
+                c, i = divmod(t, TILES_PER_CHUNK)
+                row_sum = work.tile([P, 1], F32, tag="row_sum")
+                minus_mean = work.tile([P, 1], F32, tag="minus_mean")
+                nc.vector.scalar_tensor_tensor(
+                    out=live["u", c][:, i, :],
+                    in0=live["att_ps", t][:],
+                    scalar=1.0,
+                    in1=live["u", c][:, i, :],
+                    op0=ALU.mult,
+                    op1=ALU.add,
+                    accum_out=row_sum[:],
+                )
+                nc.vector.tensor_scalar_mul(out=minus_mean[:], in0=row_sum[:], scalar1=-1.0 / FEAT)
+                live["minus_mean", t] = minus_mean
+
+        def norm_squares(t):
+            if in_range(t):
+                c, i = divmod(t, TILES_PER_CHUNK)
+                squares = work.tile([P, FEAT], BF16, tag="squares")
+                square_sum = work.tile([P, 1], F32, tag="square_sum")
+                nc.scalar.activation(
+                    out=squares[:],
+                    in_=live["u", c][:, i, :],
+                    func=ACT.Square,
+                    bias=live["minus_mean", t][:],
+                    scale=1.0,
+                    accum_out=square_sum[:],
+                )
+                live["square_sum", t] = square_sum
+
+        def norm_inv_std(t):
+            if in_range(t):
+                inv_std = work.tile([P, 1], F32, tag="inv_std")
+                nc.gpsimd.tensor_scalar(
+                    out=inv_std[:],
+                    in0=live["square_sum", t][:],
+                    scalar1=1.0 / FEAT,
+                    scalar2=LN_EPS,
+                    op0=ALU.mult,
+                    op1=ALU.add,
+                )
+                nc.gpsimd.tensor_tensor(out=inv_std[:], in0=inv_std[:], in1=minus_half[:], op=ALU.pow)
+                live["inv_std", t] = inv_std
+
+        def norm_scale(t):
+            if in_range(t):
+                c, i = divmod(t, TILES_PER_CHUNK)
+                nc.vector.tensor_scalar(
+                    out=live["u", c][:, i, :],
+                    in0=live["u", c][:, i, :],
+                    scalar1=live["minus_mean", t][:],
+                    scalar2=live["inv_std", t][:],
+                    op0=ALU.add,
+                    op1=ALU.mult,
+                )
+
+        def drive_matmul(k):
+            if in_range(k):
+                c, m = divmod(k, SLICES)
+                x_codes, x_scales = live["x_mx", c]
+                xin_ps = psum.tile([P, CHUNK_ROWS], F32, tag="xin")
+                nc.tensor.matmul_mx(
+                    out=xin_ps[:],
+                    lhsT=w_codes[:, W_IN, m * P : (m + 1) * P].bitcast(FP8X4),
+                    lhsT_scale=w_scales[:, W_IN, m * P : (m + 1) * P],
+                    rhs=x_codes[:].bitcast(FP8X4),
+                    rhs_scale=x_scales[:],
+                    start=True,
+                    stop=True,
+                )
+                live["xin_ps", k] = xin_ps
+
+        def drive_copy(k):
+            if in_range(k):
+                c, m = divmod(k, SLICES)
+                if m == 0:
+                    live["drive", c] = work.tile([P, SLICES, CHUNK_ROWS], F32, tag="drive", name="drive")
+                nc.scalar.activation(
+                    out=live["drive", c][:, m, :],
+                    in_=live["xin_ps", k][:],
+                    func=ACT.Identity,
+                    bias=shift_col[:, m : m + 1],
+                    scale=1.0,
+                )
+
+        def gate_transposes(k):
+            if in_range(k):
+                c, m = divmod(k, SLICES)
+                normed_ps = psum.tile([P, TILES_PER_CHUNK, P], F32, tag="normed")
+                for i in range(TILES_PER_CHUNK):
+                    nc.tensor.transpose(normed_ps[:, i, :], live["u", c][:, i, m * P : (m + 1) * P], ident[:])
+                live["normed_ps", k] = normed_ps
+
+        def gate_sum(k):
+            if in_range(k):
+                c, m = divmod(k, SLICES)
+                nc.vector.scalar_tensor_tensor(
+                    out=live["drive", c][:, m, :],
+                    in0=live["normed_ps", k][:].rearrange("p i r -> p (i r)"),
+                    scalar=gain_col[:, m : m + 1],
+                    in1=live["drive", c][:, m, :],
+                    op0=ALU.mult,
+                    op1=ALU.add,
+                )
+
+        def gate_tanh(k):
+            if in_range(k):
+                c, m = divmod(k, SLICES)
+                nc.scalar.activation(out=live["drive", c][:, m, :], in_=live["drive", c][:, m, :], func=ACT.Tanh)
+
+        def gate_rate(k):
+            if in_range(k):
+                c, m = divmod(k, SLICES)
+                nc.vector.tensor_scalar_mul(
+                    out=live["drive", c][:, m, :], in0=live["drive", c][:, m, :], scalar1=rate_col[:, m : m + 1]
+                )
+
+        def kept_state(t):
+            if in_range(t):
+                c, i = divmod(t, TILES_PER_CHUNK)
+                if i == 0:
+                    live["new_h", c] = work.tile([P, TILES_PER_CHUNK, FEAT], F32, tag="new_h", name="new_h")
+                nc.gpsimd.tensor_tensor(out=live["new_h", c][:, i, :], in0=live["h", c][:, i, :], in1=keep_rows[:], op=ALU.mult)
+
+        def update_transposes(t):
+            if in_range(t):
+                c, i = divmod(t, TILES_PER_CHUNK)
+                pull_ps = psum.tile([P, SLICES, P], F32, tag="pull")
+                for m in range(SLICES):
+                    nc.tensor.transpose(pull_ps[:, m, :], live["drive", c][:, m, i * P : (i + 1) * P], ident[:])
+                live["pull_ps", t] = pull_ps
+
+        def update_sum(t):
+            if in_range(t):
+                c, i = divmod(t, TILES_PER_CHUNK)
+                nc.vector.tensor_tensor(
+                    out=live["new_h", c][:, i, :],
+                    in0=live["pull_ps", t][:].rearrange("r m f -> r (m f)"),
+                    in1=live["new_h", c][:, i, :],
+                    op=ALU.add,
+                )
+                if i == TILES_PER_CHUNK - 1:
+                    nc.sync.dma_start(out=out_rows[:, chunk_rows(c), :], in_=live["new_h", c][:])
+
+        for q in range(ROW_TILES + LAG_UPDATE):
+            if (q + LOAD_AHEAD) % TILES_PER_CHUNK == 0:
+                c = (q + LOAD_AHEAD) // TILES_PER_CHUNK
+                if c >= 2:
+                    load_chunk("liq", liq_rows, c)
+                    load_chunk("x", x_rows, c)
+                load_chunk("h", h_rows, c - 1)
+            drive_matmul(q - LAG_DRIVE)
+            norm_matmul(q - LAG_NORM)
+            value_matmul(q - LAG_VALUE)
+            drive_copy(q - LAG_DRIVE)
+            value_copy(q - LAG_VALUE)
+            gate_transposes(q - LAG_GATE)
+            update_transposes(q - LAG_UPDATE)
+            entry_transposes(q)
+            value_transposes(q - LAG_VALUE)
+            residual(q - LAG_VALUE)
+            kept_state(q - LAG_KEEP)
+            norm_mean(q - LAG_NORM)
+            norm_squares(q - LAG_NORM)
+            norm_inv_std(q - LAG_NORM)
+            gate_sum(q - LAG_GATE)
+            gate_tanh(q - LAG_GATE)
+            update_sum(q - LAG_UPDATE)
+            value_quantise(q - LAG_VALUE)
+            entry_copy(q)
+            entry_quantise(q - LAG_QUANT)
+            norm_scale(q - LAG_SCALE)
+            gate_rate(q - LAG_GATE)

@@ -399,6 +399,11 @@ def tile_advancedliquidneuralnetwork_pb_t_kernel(
                 if i == TILES_PER_CHUNK - 1:
                     nc.sync.dma_start(out=out_rows[:, chunk_rows(c), :], in_=live["new_h", c][:])
 
+        def clock_passes():
+            idle_ps = psum.tile([P, FEAT], F32, tag="idle")
+            for repeat in range(2):
+                mx_rows(idle_ps, w_codes[:, W_V, 0:P], w_scales[:, W_V, 0:P], W_V)
+
         for q in range(ROW_TILES + LAG_UPDATE):
             if (q + LOAD_AHEAD) % TILES_PER_CHUNK == 0:
                 c = (q + LOAD_AHEAD) // TILES_PER_CHUNK
@@ -413,6 +418,7 @@ def tile_advancedliquidneuralnetwork_pb_t_kernel(
             value_copy(q - LAG_VALUE)
             gate_transposes(q - LAG_GATE)
             update_transposes(q - LAG_UPDATE)
+            clock_passes()
             entry_transposes(q)
             value_transposes(q - LAG_VALUE)
             residual(q - LAG_VALUE)

@@ -26,14 +26,27 @@ TAU_EPS = 1e-6
 W_IN, W_V, W_O = 0, 1, 2
 LIQ, X = 0, 1
 
-LAG_QUANT = 1
-LAG_VALUE = LAG_QUANT + 1
-LAG_NORM = LAG_VALUE + 1
-LAG_SCALE = LAG_NORM + 1
-LAG_DRIVE = LAG_QUANT + TILES_PER_CHUNK + 1
-LAG_GATE = LAG_SCALE + TILES_PER_CHUNK
-LAG_UPDATE = LAG_GATE + SLICES
-LAG_KEEP = LAG_UPDATE - TILES_PER_CHUNK
+LAG_ENTRY_COPY = 1
+LAG_ENTRY_QUANT = LAG_ENTRY_COPY + 1
+LAG_VALUE_MATMUL = LAG_ENTRY_QUANT + 1
+LAG_VALUE_COPY = LAG_VALUE_MATMUL + 1
+LAG_VALUE_TRANSPOSE = LAG_VALUE_COPY + 1
+LAG_VALUE_QUANT = LAG_VALUE_TRANSPOSE + 1
+LAG_NORM_MATMUL = LAG_VALUE_QUANT + 1
+LAG_NORM_MEAN = LAG_NORM_MATMUL + 1
+LAG_NORM_SQUARES = LAG_NORM_MEAN + 1
+LAG_NORM_INV_STD = LAG_NORM_SQUARES + 1
+LAG_NORM_SCALE = LAG_NORM_INV_STD + 1
+LAG_GATE_TRANSPOSE = LAG_NORM_SCALE + TILES_PER_CHUNK
+LAG_GATE_SUM = LAG_GATE_TRANSPOSE + 1
+LAG_GATE_TANH = LAG_GATE_SUM + 1
+LAG_GATE_RATE = LAG_GATE_TANH + 1
+LAG_UPDATE_TRANSPOSE = LAG_GATE_RATE + SLICES
+LAG_UPDATE_SUM = LAG_UPDATE_TRANSPOSE + 1
+LAG_DRIVE_COPY = LAG_GATE_SUM - 2
+LAG_DRIVE_MATMUL = LAG_DRIVE_COPY - 1
+LAG_RESIDUAL = LAG_NORM_MEAN - 1
+LAG_KEPT_STATE = LAG_UPDATE_SUM - 1
 LOAD_AHEAD = 5
 
 FLOPS = 3 * 2 * ROWS * FEAT * FEAT
@@ -70,7 +83,7 @@ def tile_advancedliquidneuralnetwork_pb_t_kernel(
         const = stack.enter_context(tc.tile_pool(name="const", bufs=1))
         loads = stack.enter_context(tc.tile_pool(name="loads", bufs=3))
         work = stack.enter_context(tc.tile_pool(name="work", bufs=3))
-        psum = stack.enter_context(tc.psum_pool(name="psum", bufs=1))
+        psum = stack.enter_context(tc.psum_pool(name="psum", bufs=8))
 
         live = {}
 
@@ -79,7 +92,7 @@ def tile_advancedliquidneuralnetwork_pb_t_kernel(
 
         def load_chunk(name, rows, c):
             if c < CHUNKS:
-                live[name, c] = loads.tile([P, TILES_PER_CHUNK, FEAT], BF16, tag=name, name=name, bufs=4 if name == "h" else 3)
+                live[name, c] = loads.tile([P, TILES_PER_CHUNK, FEAT], BF16, tag=name, name=name, bufs=4 if name == "liq" else 3)
                 nc.sync.dma_start(out=live[name, c][:], in_=rows[:, chunk_rows(c), :])
 
         w_codes = const.tile([P, 3, FEAT], U32, align_bytes=64)
@@ -107,7 +120,6 @@ def tile_advancedliquidneuralnetwork_pb_t_kernel(
         load_weight_words(W_IN)
         load_chunk("liq", liq_rows, 1)
         load_chunk("x", x_rows, 1)
-        load_chunk("h", h_rows, 0)
 
         ident = const.tile([P, P], F32)
         make_identity(nc, ident[:])
@@ -127,7 +139,7 @@ def tile_advancedliquidneuralnetwork_pb_t_kernel(
         tau_rows = const.tile([P, FEAT], BF16)
         nc.scalar.dma_start(out=tau_rows[:], in_=tau.partition_broadcast(P))
 
-        vec_ps = psum.tile([P, P], BF16, tag="words")
+        vec_ps = psum.tile([P, P], BF16, tag="bank")
         nc.tensor.transpose(vec_ps[:], vec_rows[:], ident_bf[:])
         vec_cols = const.tile([P, 4 * SLICES], F32)
         nc.vector.tensor_copy(out=vec_cols[:], in_=vec_ps[:, 0 : 4 * SLICES])
@@ -163,7 +175,7 @@ def tile_advancedliquidneuralnetwork_pb_t_kernel(
         def entry_transposes(t):
             if in_range(t):
                 c, i = divmod(t, TILES_PER_CHUNK)
-                planes = psum.tile([P, 2, 2, P], F32, tag="words")
+                planes = psum.tile([P, 2, 2, P], F32, tag="bank")
                 for s, name in ((LIQ, "liq"), (X, "x")):
                     words = live[name, c][:, i, :].bitcast(F32)
                     for u in range(2):
@@ -192,8 +204,8 @@ def tile_advancedliquidneuralnetwork_pb_t_kernel(
                 )
                 live["liq_mx", t] = (liq_codes, liq_scales)
                 if i == 0:
-                    x_codes = work.tile([P, CHUNK_ROWS], U32, tag="x_codes", align_bytes=64)
-                    x_scales = work.tile([P, CHUNK_ROWS], U8, tag="x_scales", align_bytes=64)
+                    x_codes = work.tile([P, CHUNK_ROWS], U32, tag="x_codes", align_bytes=64, bufs=4)
+                    x_scales = work.tile([P, CHUNK_ROWS], U8, tag="x_scales", align_bytes=64, bufs=4)
                     live["x_mx", c] = (x_codes, x_scales)
                 x_codes, x_scales = live["x_mx", c]
                 nc.vector.quantize_mx(
@@ -205,7 +217,7 @@ def tile_advancedliquidneuralnetwork_pb_t_kernel(
         def value_matmul(t):
             if in_range(t):
                 liq_codes, liq_scales = live["liq_mx", t]
-                v_ps = psum.tile([P, FEAT], F32, tag="v")
+                v_ps = psum.tile([P, FEAT], F32, tag="bank")
                 mx_rows(v_ps, liq_codes[:], liq_scales[:], W_V)
                 live["v_ps", t] = v_ps
 
@@ -218,7 +230,7 @@ def tile_advancedliquidneuralnetwork_pb_t_kernel(
         def value_transposes(t):
             if in_range(t):
                 v_planes = live["v_planes", t]
-                vt_ps = psum.tile([P, PACK, P], F32, tag="vt")
+                vt_ps = psum.tile([P, PACK, P], F32, tag="bank")
                 for j in range(PACK):
                     nc.tensor.transpose(vt_ps[:, j, :], v_planes[:, j, :], ident[:])
                 live["vt_ps", t] = vt_ps
@@ -249,7 +261,7 @@ def tile_advancedliquidneuralnetwork_pb_t_kernel(
         def norm_matmul(t):
             if in_range(t):
                 v_codes, v_scales = live["v_mx", t]
-                att_ps = psum.tile([P, FEAT], F32, tag="att")
+                att_ps = psum.tile([P, FEAT], F32, tag="bank")
                 mx_rows(att_ps, v_codes[:], v_scales[:], W_O)
                 live["att_ps", t] = att_ps
 
@@ -257,7 +269,7 @@ def tile_advancedliquidneuralnetwork_pb_t_kernel(
             if in_range(t):
                 c, i = divmod(t, TILES_PER_CHUNK)
                 row_sum = work.tile([P, 1], F32, tag="row_sum")
-                minus_mean = work.tile([P, 1], F32, tag="minus_mean")
+                minus_mean = work.tile([P, 1], F32, tag="minus_mean", bufs=5)
                 nc.vector.scalar_tensor_tensor(
                     out=live["u", c][:, i, :],
                     in0=live["att_ps", t][:],
@@ -315,7 +327,7 @@ def tile_advancedliquidneuralnetwork_pb_t_kernel(
             if in_range(k):
                 c, m = divmod(k, SLICES)
                 x_codes, x_scales = live["x_mx", c]
-                xin_ps = psum.tile([P, CHUNK_ROWS], F32, tag="xin")
+                xin_ps = psum.tile([P, CHUNK_ROWS], F32, tag="bank")
                 nc.tensor.matmul_mx(
                     out=xin_ps[:],
                     lhsT=w_codes[:, W_IN, m * P : (m + 1) * P].bitcast(FP8X4),
@@ -343,7 +355,7 @@ def tile_advancedliquidneuralnetwork_pb_t_kernel(
         def gate_transposes(k):
             if in_range(k):
                 c, m = divmod(k, SLICES)
-                normed_ps = psum.tile([P, TILES_PER_CHUNK, P], F32, tag="normed")
+                normed_ps = psum.tile([P, TILES_PER_CHUNK, P], F32, tag="bank")
                 for i in range(TILES_PER_CHUNK):
                     nc.tensor.transpose(normed_ps[:, i, :], live["u", c][:, i, m * P : (m + 1) * P], ident[:])
                 live["normed_ps", k] = normed_ps
@@ -382,7 +394,7 @@ def tile_advancedliquidneuralnetwork_pb_t_kernel(
         def update_transposes(t):
             if in_range(t):
                 c, i = divmod(t, TILES_PER_CHUNK)
-                pull_ps = psum.tile([P, SLICES, P], F32, tag="pull")
+                pull_ps = psum.tile([P, SLICES, P], F32, tag="bank")
                 for m in range(SLICES):
                     nc.tensor.transpose(pull_ps[:, m, :], live["drive", c][:, m, i * P : (i + 1) * P], ident[:])
                 live["pull_ps", t] = pull_ps
@@ -399,38 +411,33 @@ def tile_advancedliquidneuralnetwork_pb_t_kernel(
                 if i == TILES_PER_CHUNK - 1:
                     nc.sync.dma_start(out=out_rows[:, chunk_rows(c), :], in_=live["new_h", c][:])
 
-        def clock_passes():
-            idle_ps = psum.tile([P, FEAT], F32, tag="idle")
-            for repeat in range(2):
-                mx_rows(idle_ps, w_codes[:, W_V, 0:P], w_scales[:, W_V, 0:P], W_V)
-
-        for q in range(ROW_TILES + LAG_UPDATE):
-            if (q + LOAD_AHEAD) % TILES_PER_CHUNK == 0:
-                c = (q + LOAD_AHEAD) // TILES_PER_CHUNK
-                if c >= 2:
-                    load_chunk("liq", liq_rows, c)
-                    load_chunk("x", x_rows, c)
-                load_chunk("h", h_rows, c - 1)
-            drive_matmul(q - LAG_DRIVE)
-            norm_matmul(q - LAG_NORM)
-            value_matmul(q - LAG_VALUE)
-            drive_copy(q - LAG_DRIVE)
-            value_copy(q - LAG_VALUE)
-            gate_transposes(q - LAG_GATE)
-            update_transposes(q - LAG_UPDATE)
-            clock_passes()
+        for q in range(ROW_TILES + LAG_UPDATE_SUM):
+            c, i = divmod(q + LOAD_AHEAD, TILES_PER_CHUNK)
+            if i == 0 and c >= 2:
+                load_chunk("liq", liq_rows, c)
+                load_chunk("x", x_rows, c)
+            c, i = divmod(q + LOAD_AHEAD - LAG_KEPT_STATE, TILES_PER_CHUNK)
+            if i == 0 and c >= 0:
+                load_chunk("h", h_rows, c)
+            drive_matmul(q - LAG_DRIVE_MATMUL)
+            norm_matmul(q - LAG_NORM_MATMUL)
+            value_matmul(q - LAG_VALUE_MATMUL)
+            gate_transposes(q - LAG_GATE_TRANSPOSE)
+            update_transposes(q - LAG_UPDATE_TRANSPOSE)
+            value_transposes(q - LAG_VALUE_TRANSPOSE)
             entry_transposes(q)
-            value_transposes(q - LAG_VALUE)
-            residual(q - LAG_VALUE)
-            kept_state(q - LAG_KEEP)
-            norm_mean(q - LAG_NORM)
-            norm_squares(q - LAG_NORM)
-            norm_inv_std(q - LAG_NORM)
-            gate_sum(q - LAG_GATE)
-            gate_tanh(q - LAG_GATE)
-            update_sum(q - LAG_UPDATE)
-            value_quantise(q - LAG_VALUE)
-            entry_copy(q)
-            entry_quantise(q - LAG_QUANT)
-            norm_scale(q - LAG_SCALE)
-            gate_rate(q - LAG_GATE)
+            drive_copy(q - LAG_DRIVE_COPY)
+            value_copy(q - LAG_VALUE_COPY)
+            norm_squares(q - LAG_NORM_SQUARES)
+            gate_tanh(q - LAG_GATE_TANH)
+            entry_copy(q - LAG_ENTRY_COPY)
+            norm_inv_std(q - LAG_NORM_INV_STD)
+            residual(q - LAG_RESIDUAL)
+            kept_state(q - LAG_KEPT_STATE)
+            norm_mean(q - LAG_NORM_MEAN)
+            gate_sum(q - LAG_GATE_SUM)
+            update_sum(q - LAG_UPDATE_SUM)
+            value_quantise(q - LAG_VALUE_QUANT)
+            entry_quantise(q - LAG_ENTRY_QUANT)
+            norm_scale(q - LAG_NORM_SCALE)
+            gate_rate(q - LAG_GATE_RATE)

@@ -389,7 +389,7 @@ def tile_advancedliquidneuralnetwork_pb_t_kernel(
                 c, i = divmod(t, TILES_PER_CHUNK)
                 if i == 0:
                     live["new_h", c] = work.tile([P, TILES_PER_CHUNK, FEAT], F32, tag="new_h", name="new_h")
-                nc.gpsimd.tensor_tensor(out=live["new_h", c][:, i, :], in0=live["h", c][:, i, :], in1=keep_rows[:], op=ALU.mult)
+                nc.vector.tensor_tensor(out=live["new_h", c][:, i, :], in0=live["h", c][:, i, :], in1=keep_rows[:], op=ALU.mult)
 
         def update_transposes(t):
             if in_range(t):
@@ -433,7 +433,6 @@ def tile_advancedliquidneuralnetwork_pb_t_kernel(
             entry_copy(q - LAG_ENTRY_COPY)
             norm_inv_std(q - LAG_NORM_INV_STD)
             residual(q - LAG_RESIDUAL)
-            kept_state(q - LAG_KEPT_STATE)
             norm_mean(q - LAG_NORM_MEAN)
             gate_sum(q - LAG_GATE_SUM)
             update_sum(q - LAG_UPDATE_SUM)
@@ -441,3 +440,4 @@ def tile_advancedliquidneuralnetwork_pb_t_kernel(
             entry_quantise(q - LAG_ENTRY_QUANT)
             norm_scale(q - LAG_NORM_SCALE)
             gate_rate(q - LAG_GATE_RATE)
+            kept_state(q - LAG_KEPT_STATE)

@@ -31,9 +31,11 @@ LAG_ENTRY_QUANT = LAG_ENTRY_COPY + 1
 LAG_VALUE_MATMUL = LAG_ENTRY_QUANT + 1
 LAG_VALUE_COPY = LAG_VALUE_MATMUL + 1
 LAG_VALUE_TRANSPOSE = LAG_VALUE_COPY + 1
-LAG_VALUE_QUANT = LAG_VALUE_TRANSPOSE + 1
+LAG_VALUE_BIAS = LAG_VALUE_TRANSPOSE + 1
+LAG_VALUE_QUANT = LAG_VALUE_BIAS + 1
 LAG_NORM_MATMUL = LAG_VALUE_QUANT + 1
-LAG_NORM_MEAN = LAG_NORM_MATMUL + 1
+LAG_NORM_SUM = LAG_NORM_MATMUL + 1
+LAG_NORM_MEAN = LAG_NORM_SUM + 1
 LAG_NORM_SQUARES = LAG_NORM_MEAN + 1
 LAG_NORM_INV_STD = LAG_NORM_SQUARES + 1
 LAG_NORM_SCALE = LAG_NORM_INV_STD + 1
@@ -45,9 +47,10 @@ LAG_UPDATE_TRANSPOSE = LAG_GATE_RATE + SLICES
 LAG_UPDATE_SUM = LAG_UPDATE_TRANSPOSE + 1
 LAG_DRIVE_COPY = LAG_GATE_SUM - 2
 LAG_DRIVE_MATMUL = LAG_DRIVE_COPY - 1
-LAG_RESIDUAL = LAG_NORM_MEAN - 1
+LAG_RESIDUAL = LAG_NORM_SUM - 1
 LAG_KEPT_STATE = LAG_UPDATE_SUM - 1
-LOAD_AHEAD = 5
+LOAD_AHEAD = 4
+CONSTANTS_ROUND = 8
 
 FLOPS = 3 * 2 * ROWS * FEAT * FEAT
 
@@ -91,72 +94,67 @@ def tile_advancedliquidneuralnetwork_pb_t_kernel(
             return slice(c * TILES_PER_CHUNK, (c + 1) * TILES_PER_CHUNK)
 
         def load_chunk(name, rows, c):
-            if c < CHUNKS:
+            if 0 <= c < CHUNKS:
                 live[name, c] = loads.tile([P, TILES_PER_CHUNK, FEAT], BF16, tag=name, name=name, bufs=4 if name == "liq" else 3)
                 nc.sync.dma_start(out=live[name, c][:], in_=rows[:, chunk_rows(c), :])
 
         w_codes = const.tile([P, 3, FEAT], U32, align_bytes=64)
         w_scales = const.tile([P, 3, FEAT], U8, align_bytes=64)
         nc.vector.memset(w_scales[:].bitcast(I32), 0)
-        given = {W_V: (W_v_words, W_v_scales), W_O: (W_o_words, W_o_scales), W_IN: (W_in_words, W_in_scales)}
-        for w in (W_V, W_O, W_IN):
-            scale_rows = given[w][1].rearrange("g q n -> (g q) n").bitcast(I32)
+
+        def load_weight(w, words, scales):
+            nc.sync.dma_start(
+                out=w_codes[:, w, :].bitcast(I32), in_=words.rearrange("g p n t -> (g p) (n t)").bitcast(I32)
+            )
+            scale_rows = scales.rearrange("g q n -> (g q) n").bitcast(I32)
             for quadrant in range(4):
                 nc.sync.dma_start(
                     out=w_scales[32 * quadrant : 32 * quadrant + 4, w, :].bitcast(I32),
                     in_=scale_rows[4 * quadrant : 4 * quadrant + 4, :],
                 )
 
-        def load_weight_words(w):
-            nc.sync.dma_start(
-                out=w_codes[:, w, :].bitcast(I32),
-                in_=given[w][0].rearrange("g p n t -> (g p) (n t)").bitcast(I32),
-            )
+        bv_words = const.tile([P, PACK], BF16)
+        bo_rows = const.tile([P, FEAT], BF16)
+        tau_rows = const.tile([P, FEAT], BF16)
+        vec_rows = const.tile([P, P], BF16)
+        nc.vector.memset(vec_rows[:], 0.0)
 
         load_chunk("liq", liq_rows, 0)
         load_chunk("x", x_rows, 0)
-        load_weight_words(W_V)
-        load_weight_words(W_O)
-        load_weight_words(W_IN)
-        load_chunk("liq", liq_rows, 1)
-        load_chunk("x", x_rows, 1)
+        load_weight(W_V, W_v_words, W_v_scales)
+        nc.sync.dma_start(out=bv_words[:], in_=b_v.rearrange("(p t) -> p t", t=PACK))
+        load_weight(W_O, W_o_words, W_o_scales)
+        nc.sync.dma_start(out=bo_rows[:], in_=b_o.partition_broadcast(P))
+        load_weight(W_IN, W_in_words, W_in_scales)
+        for i, vec in enumerate((b_in, beta_att, g_att, tau)):
+            nc.sync.dma_start(out=vec_rows[SLICES * i : SLICES * (i + 1), :], in_=vec.rearrange("(m p) -> m p", p=P))
+        nc.sync.dma_start(out=tau_rows[:], in_=tau.partition_broadcast(P))
 
         ident = const.tile([P, P], F32)
         make_identity(nc, ident[:])
         ident_bf = const.tile([P, P], BF16)
         make_identity(nc, ident_bf[:])
-
-        vec_rows = const.tile([P, P], BF16)
-        nc.vector.memset(vec_rows[:], 0.0)
-        for i, vec in enumerate((b_in, beta_att, g_att, tau)):
-            nc.scalar.dma_start(
-                out=vec_rows[SLICES * i : SLICES * (i + 1), :], in_=vec.rearrange("(m p) -> m p", p=P)
-            )
-        bv_words = const.tile([P, PACK], BF16)
-        nc.scalar.dma_start(out=bv_words[:], in_=b_v.rearrange("(p t) -> p t", t=PACK))
-        bo_rows = const.tile([P, FEAT], BF16)
-        nc.scalar.dma_start(out=bo_rows[:], in_=b_o.partition_broadcast(P))
-        tau_rows = const.tile([P, FEAT], BF16)
-        nc.scalar.dma_start(out=tau_rows[:], in_=tau.partition_broadcast(P))
-
-        vec_ps = psum.tile([P, P], BF16, tag="bank")
-        nc.tensor.transpose(vec_ps[:], vec_rows[:], ident_bf[:])
-        vec_cols = const.tile([P, 4 * SLICES], F32)
-        nc.vector.tensor_copy(out=vec_cols[:], in_=vec_ps[:, 0 : 4 * SLICES])
-        shift_col = const.tile([P, SLICES], F32)
-        nc.vector.tensor_add(out=shift_col[:], in0=vec_cols[:, 0:SLICES], in1=vec_cols[:, SLICES : 2 * SLICES])
-        gain_col = vec_cols[:, 2 * SLICES : 3 * SLICES]
-        rate_col = const.tile([P, SLICES], F32)
-        nc.vector.tensor_scalar_add(out=rate_col[:], in0=vec_cols[:, 3 * SLICES : 4 * SLICES], scalar1=TAU_EPS)
-        nc.vector.reciprocal(out=rate_col[:], in_=rate_col[:])
-        keep_rows = const.tile([P, FEAT], F32)
-        nc.vector.tensor_scalar_add(out=keep_rows[:], in0=tau_rows[:], scalar1=TAU_EPS)
-        nc.vector.reciprocal(out=keep_rows[:], in_=keep_rows[:])
-        nc.vector.tensor_scalar(
-            out=keep_rows[:], in0=keep_rows[:], scalar1=-1.0, scalar2=1.0, op0=ALU.mult, op1=ALU.add
-        )
         minus_half = const.tile([P, 1], F32)
         nc.vector.memset(minus_half[:], -0.5)
+
+        vec_cols = const.tile([P, 4 * SLICES], F32)
+        shift_col = const.tile([P, SLICES], F32)
+        gain_col = vec_cols[:, 2 * SLICES : 3 * SLICES]
+        rate_col = const.tile([P, SLICES], F32)
+        keep_rows = const.tile([P, FEAT], F32)
+
+        def feature_constants():
+            vec_ps = psum.tile([P, P], BF16, tag="bank")
+            nc.tensor.transpose(vec_ps[:], vec_rows[:], ident_bf[:])
+            nc.vector.tensor_copy(out=vec_cols[:], in_=vec_ps[:, 0 : 4 * SLICES])
+            nc.vector.tensor_scalar_add(out=keep_rows[:], in0=tau_rows[:], scalar1=TAU_EPS)
+            nc.vector.tensor_add(out=shift_col[:], in0=vec_cols[:, 0:SLICES], in1=vec_cols[:, SLICES : 2 * SLICES])
+            nc.vector.reciprocal(out=keep_rows[:], in_=keep_rows[:])
+            nc.vector.tensor_scalar_add(out=rate_col[:], in0=vec_cols[:, 3 * SLICES : 4 * SLICES], scalar1=TAU_EPS)
+            nc.vector.tensor_scalar(
+                out=keep_rows[:], in0=keep_rows[:], scalar1=-1.0, scalar2=1.0, op0=ALU.mult, op1=ALU.add
+            )
+            nc.vector.reciprocal(out=rate_col[:], in_=rate_col[:])
 
         def in_range(t):
             return 0 <= t < ROW_TILES
@@ -164,8 +162,8 @@ def tile_advancedliquidneuralnetwork_pb_t_kernel(
         def mx_rows(acc, codes, scales, w):
             nc.tensor.matmul_mx(
                 out=acc[:],
-                lhsT=codes.bitcast(FP8X4),
-                lhsT_scale=scales,
+                lhsT=codes[:].bitcast(FP8X4),
+                lhsT_scale=scales[:],
                 rhs=w_codes[:, w, :].bitcast(FP8X4),
                 rhs_scale=w_scales[:, w, :],
                 start=True,
@@ -204,8 +202,8 @@ def tile_advancedliquidneuralnetwork_pb_t_kernel(
                 )
                 live["liq_mx", t] = (liq_codes, liq_scales)
                 if i == 0:
-                    x_codes = work.tile([P, CHUNK_ROWS], U32, tag="x_codes", align_bytes=64, bufs=4)
-                    x_scales = work.tile([P, CHUNK_ROWS], U8, tag="x_scales", align_bytes=64, bufs=4)
+                    x_codes = work.tile([P, CHUNK_ROWS], U32, tag="x_codes", align_bytes=64, bufs=5)
+                    x_scales = work.tile([P, CHUNK_ROWS], U8, tag="x_scales", align_bytes=64, bufs=5)
                     live["x_mx", c] = (x_codes, x_scales)
                 x_codes, x_scales = live["x_mx", c]
                 nc.vector.quantize_mx(
@@ -216,38 +214,44 @@ def tile_advancedliquidneuralnetwork_pb_t_kernel(
 
         def value_matmul(t):
             if in_range(t):
-                liq_codes, liq_scales = live["liq_mx", t]
                 v_ps = psum.tile([P, FEAT], F32, tag="bank")
-                mx_rows(v_ps, liq_codes[:], liq_scales[:], W_V)
+                mx_rows(v_ps, live["liq_mx", t][0], live["liq_mx", t][1], W_V)
                 live["v_ps", t] = v_ps
 
         def value_copy(t):
             if in_range(t):
                 v_planes = work.tile([P, PACK, P], F32, tag="v_planes")
-                nc.scalar.copy(out=v_planes[:], in_=live["v_ps", t][:].rearrange("r (p t) -> r t p", t=PACK))
+                nc.scalar.copy(
+                    out=v_planes[:].rearrange("r j p -> r p j"), in_=live["v_ps", t][:].rearrange("r (p j) -> r p j", j=PACK)
+                )
                 live["v_planes", t] = v_planes
 
         def value_transposes(t):
             if in_range(t):
-                v_planes = live["v_planes", t]
                 vt_ps = psum.tile([P, PACK, P], F32, tag="bank")
                 for j in range(PACK):
-                    nc.tensor.transpose(vt_ps[:, j, :], v_planes[:, j, :], ident[:])
+                    nc.tensor.transpose(vt_ps[:, j, :], live["v_planes", t][:, j, :], ident[:])
                 live["vt_ps", t] = vt_ps
 
-        def value_quantise(t):
+        def value_bias(t):
             if in_range(t):
                 grouped = work.tile([P, P, PACK], BF16, tag="v_grouped", align_bytes=64)
                 nc.vector.tensor_tensor(
                     out=grouped[:],
-                    in0=live["vt_ps", t][:].rearrange("p t r -> p r t"),
+                    in0=live["vt_ps", t][:].rearrange("p j r -> p r j"),
                     in1=bv_words[:].unsqueeze(1).to_broadcast([P, P, PACK]),
                     op=ALU.add,
                 )
+                live["v_grouped", t] = grouped
+
+        def value_quantise(t):
+            if in_range(t):
                 v_codes = work.tile([P, P], U32, tag="v_codes", align_bytes=64)
                 v_scales = work.tile([P, P], U8, tag="v_scales", align_bytes=64)
                 nc.vector.quantize_mx(
-                    out=v_codes[:].bitcast(FP8X4), scales=v_scales[:], in_=grouped[:].rearrange("p r t -> p (r t)")
+                    out=v_codes[:].bitcast(FP8X4),
+                    scales=v_scales[:],
+                    in_=live["v_grouped", t][:].rearrange("p r j -> p (r j)"),
                 )
                 live["v_mx", t] = (v_codes, v_scales)
 
@@ -255,21 +259,19 @@ def tile_advancedliquidneuralnetwork_pb_t_kernel(
             if in_range(t):
                 c, i = divmod(t, TILES_PER_CHUNK)
                 if i == 0:
-                    live["u", c] = work.tile([P, TILES_PER_CHUNK, FEAT], F32, tag="u", name="u")
-                nc.gpsimd.tensor_tensor(out=live["u", c][:, i, :], in0=live["liq", c][:, i, :], in1=bo_rows[:], op=ALU.add)
+                    live["u", c] = work.tile([P, TILES_PER_CHUNK, FEAT], F32, tag="u", name="u", bufs=4)
+                nc.vector.tensor_tensor(out=live["u", c][:, i, :], in0=live["liq", c][:, i, :], in1=bo_rows[:], op=ALU.add)
 
         def norm_matmul(t):
             if in_range(t):
-                v_codes, v_scales = live["v_mx", t]
                 att_ps = psum.tile([P, FEAT], F32, tag="bank")
-                mx_rows(att_ps, v_codes[:], v_scales[:], W_O)
+                mx_rows(att_ps, live["v_mx", t][0], live["v_mx", t][1], W_O)
                 live["att_ps", t] = att_ps
 
-        def norm_mean(t):
+        def norm_sum(t):
             if in_range(t):
                 c, i = divmod(t, TILES_PER_CHUNK)
                 row_sum = work.tile([P, 1], F32, tag="row_sum")
-                minus_mean = work.tile([P, 1], F32, tag="minus_mean", bufs=5)
                 nc.vector.scalar_tensor_tensor(
                     out=live["u", c][:, i, :],
                     in0=live["att_ps", t][:],
@@ -279,7 +281,14 @@ def tile_advancedliquidneuralnetwork_pb_t_kernel(
                     op1=ALU.add,
                     accum_out=row_sum[:],
                 )
-                nc.vector.tensor_scalar_mul(out=minus_mean[:], in0=row_sum[:], scalar1=-1.0 / FEAT)
+                live["row_sum", t] = row_sum
+
+        def norm_mean(t):
+            if in_range(t):
+                minus_mean = work.tile([P, 1], F32, tag="minus_mean", bufs=4)
+                nc.gpsimd.tensor_scalar(
+                    out=minus_mean[:], in0=live["row_sum", t][:], scalar1=-1.0 / FEAT, scalar2=0.0, op0=ALU.mult, op1=ALU.add
+                )
                 live["minus_mean", t] = minus_mean
 
         def norm_squares(t):
@@ -300,27 +309,24 @@ def tile_advancedliquidneuralnetwork_pb_t_kernel(
         def norm_inv_std(t):
             if in_range(t):
                 inv_std = work.tile([P, 1], F32, tag="inv_std")
+                offset = work.tile([P, 1], F32, tag="offset")
                 nc.gpsimd.tensor_scalar(
-                    out=inv_std[:],
-                    in0=live["square_sum", t][:],
-                    scalar1=1.0 / FEAT,
-                    scalar2=LN_EPS,
-                    op0=ALU.mult,
-                    op1=ALU.add,
+                    out=inv_std[:], in0=live["square_sum", t][:], scalar1=1.0 / FEAT, scalar2=LN_EPS, op0=ALU.mult, op1=ALU.add
                 )
                 nc.gpsimd.tensor_tensor(out=inv_std[:], in0=inv_std[:], in1=minus_half[:], op=ALU.pow)
+                nc.gpsimd.tensor_tensor(out=offset[:], in0=live["minus_mean", t][:], in1=inv_std[:], op=ALU.mult)
                 live["inv_std", t] = inv_std
+                live["offset", t] = offset
 
         def norm_scale(t):
             if in_range(t):
                 c, i = divmod(t, TILES_PER_CHUNK)
-                nc.vector.tensor_scalar(
+                nc.scalar.activation(
                     out=live["u", c][:, i, :],
-                    in0=live["u", c][:, i, :],
-                    scalar1=live["minus_mean", t][:],
-                    scalar2=live["inv_std", t][:],
-                    op0=ALU.add,
-                    op1=ALU.mult,
+                    in_=live["u", c][:, i, :],
+                    func=ACT.Identity,
+                    bias=live["offset", t][:],
+                    scale=live["inv_std", t][:],
                 )
 
         def drive_matmul(k):
@@ -389,7 +395,7 @@ def tile_advancedliquidneuralnetwork_pb_t_kernel(
                 c, i = divmod(t, TILES_PER_CHUNK)
                 if i == 0:
                     live["new_h", c] = work.tile([P, TILES_PER_CHUNK, FEAT], F32, tag="new_h", name="new_h")
-                nc.vector.tensor_tensor(out=live["new_h", c][:, i, :], in0=live["h", c][:, i, :], in1=keep_rows[:], op=ALU.mult)
+                nc.gpsimd.tensor_tensor(out=live["new_h", c][:, i, :], in0=live["h", c][:, i, :], in1=keep_rows[:], op=ALU.mult)
 
         def update_transposes(t):
             if in_range(t):
@@ -413,12 +419,12 @@ def tile_advancedliquidneuralnetwork_pb_t_kernel(
 
         for q in range(ROW_TILES + LAG_UPDATE_SUM):
             c, i = divmod(q + LOAD_AHEAD, TILES_PER_CHUNK)
-            if i == 0 and c >= 2:
+            if i == 0:
                 load_chunk("liq", liq_rows, c)
                 load_chunk("x", x_rows, c)
-            c, i = divmod(q + LOAD_AHEAD - LAG_KEPT_STATE, TILES_PER_CHUNK)
-            if i == 0 and c >= 0:
-                load_chunk("h", h_rows, c)
+                load_chunk("h", h_rows, c - LAG_KEPT_STATE // TILES_PER_CHUNK)
+            if q == CONSTANTS_ROUND:
+                feature_constants()
             drive_matmul(q - LAG_DRIVE_MATMUL)
             norm_matmul(q - LAG_NORM_MATMUL)
             value_matmul(q - LAG_VALUE_MATMUL)
@@ -429,15 +435,17 @@ def tile_advancedliquidneuralnetwork_pb_t_kernel(
             drive_copy(q - LAG_DRIVE_COPY)
             value_copy(q - LAG_VALUE_COPY)
             norm_squares(q - LAG_NORM_SQUARES)
+            norm_scale(q - LAG_NORM_SCALE)
             gate_tanh(q - LAG_GATE_TANH)
             entry_copy(q - LAG_ENTRY_COPY)
-            norm_inv_std(q - LAG_NORM_INV_STD)
-            residual(q - LAG_RESIDUAL)
             norm_mean(q - LAG_NORM_MEAN)
+            norm_inv_std(q - LAG_NORM_INV_STD)
+            kept_state(q - LAG_KEPT_STATE)
+            norm_sum(q - LAG_NORM_SUM)
             gate_sum(q - LAG_GATE_SUM)
             update_sum(q - LAG_UPDATE_SUM)
+            value_bias(q - LAG_VALUE_BIAS)
             value_quantise(q - LAG_VALUE_QUANT)
             entry_quantise(q - LAG_ENTRY_QUANT)
-            norm_scale(q - LAG_NORM_SCALE)
             gate_rate(q - LAG_GATE_RATE)
-            kept_state(q - LAG_KEPT_STATE)
+            residual(q - LAG_RESIDUAL)

@@ -42,9 +42,8 @@ LAG_NORM_SCALE = LAG_NORM_INV_STD + 1
 LAG_GATE_TRANSPOSE = LAG_NORM_SCALE + TILES_PER_CHUNK
 LAG_GATE_SUM = LAG_GATE_TRANSPOSE + 1
 LAG_GATE_TANH = LAG_GATE_SUM + 1
-LAG_GATE_RATE = LAG_GATE_TANH + 1
-LAG_UPDATE_TRANSPOSE = LAG_GATE_RATE + SLICES
-LAG_UPDATE_SUM = LAG_UPDATE_TRANSPOSE + 1
+LAG_UPDATE_PRODUCT = LAG_GATE_TANH + SLICES
+LAG_UPDATE_SUM = LAG_UPDATE_PRODUCT + 1
 LAG_DRIVE_COPY = LAG_GATE_SUM - 2
 LAG_DRIVE_MATMUL = LAG_DRIVE_COPY - 1
 LAG_RESIDUAL = LAG_NORM_SUM - 1
@@ -141,6 +140,7 @@ def tile_advancedliquidneuralnetwork_pb_t_kernel(
         shift_col = const.tile([P, SLICES], F32)
         gain_col = vec_cols[:, 2 * SLICES : 3 * SLICES]
         rate_col = const.tile([P, SLICES], F32)
+        rate_diag = const.tile([P, SLICES, P], F32)
         keep_rows = const.tile([P, FEAT], F32)
 
         def feature_constants():
@@ -155,6 +155,8 @@ def tile_advancedliquidneuralnetwork_pb_t_kernel(
                 out=keep_rows[:], in0=keep_rows[:], scalar1=-1.0, scalar2=1.0, op0=ALU.mult, op1=ALU.add
             )
             nc.vector.reciprocal(out=rate_col[:], in_=rate_col[:])
+            for m in range(SLICES):
+                nc.vector.tensor_scalar_mul(out=rate_diag[:, m, :], in0=ident[:], scalar1=rate_col[:, m : m + 1])
 
         def in_range(t):
             return 0 <= t < ROW_TILES
@@ -383,13 +385,6 @@ def tile_advancedliquidneuralnetwork_pb_t_kernel(
                 c, m = divmod(k, SLICES)
                 nc.scalar.activation(out=live["drive", c][:, m, :], in_=live["drive", c][:, m, :], func=ACT.Tanh)
 
-        def gate_rate(k):
-            if in_range(k):
-                c, m = divmod(k, SLICES)
-                nc.vector.tensor_scalar_mul(
-                    out=live["drive", c][:, m, :], in0=live["drive", c][:, m, :], scalar1=rate_col[:, m : m + 1]
-                )
-
         def kept_state(t):
             if in_range(t):
                 c, i = divmod(t, TILES_PER_CHUNK)
@@ -397,12 +392,18 @@ def tile_advancedliquidneuralnetwork_pb_t_kernel(
                     live["new_h", c] = work.tile([P, TILES_PER_CHUNK, FEAT], F32, tag="new_h", name="new_h")
                 nc.gpsimd.tensor_tensor(out=live["new_h", c][:, i, :], in0=live["h", c][:, i, :], in1=keep_rows[:], op=ALU.mult)
 
-        def update_transposes(t):
+        def update_products(t):
             if in_range(t):
                 c, i = divmod(t, TILES_PER_CHUNK)
                 pull_ps = psum.tile([P, SLICES, P], F32, tag="bank")
                 for m in range(SLICES):
-                    nc.tensor.transpose(pull_ps[:, m, :], live["drive", c][:, m, i * P : (i + 1) * P], ident[:])
+                    nc.tensor.matmul(
+                        out=pull_ps[:, m, :],
+                        lhsT=live["drive", c][:, m, i * P : (i + 1) * P],
+                        rhs=rate_diag[:, m, :],
+                        start=True,
+                        stop=True,
+                    )
                 live["pull_ps", t] = pull_ps
 
         def update_sum(t):
@@ -429,8 +430,8 @@ def tile_advancedliquidneuralnetwork_pb_t_kernel(
             norm_matmul(q - LAG_NORM_MATMUL)
             value_matmul(q - LAG_VALUE_MATMUL)
             gate_transposes(q - LAG_GATE_TRANSPOSE)
-            update_transposes(q - LAG_UPDATE_TRANSPOSE)
             value_transposes(q - LAG_VALUE_TRANSPOSE)
+            update_products(q - LAG_UPDATE_PRODUCT)
             entry_transposes(q)
             drive_copy(q - LAG_DRIVE_COPY)
             value_copy(q - LAG_VALUE_COPY)
@@ -443,9 +444,8 @@ def tile_advancedliquidneuralnetwork_pb_t_kernel(
             kept_state(q - LAG_KEPT_STATE)
             norm_sum(q - LAG_NORM_SUM)
             gate_sum(q - LAG_GATE_SUM)
-            update_sum(q - LAG_UPDATE_SUM)
             value_bias(q - LAG_VALUE_BIAS)
+            update_sum(q - LAG_UPDATE_SUM)
             value_quantise(q - LAG_VALUE_QUANT)
             entry_quantise(q - LAG_ENTRY_QUANT)
-            gate_rate(q - LAG_GATE_RATE)
             residual(q - LAG_RESIDUAL)

@@ -29,9 +29,7 @@ LIQ, X = 0, 1
 LAG_ENTRY_COPY = 1
 LAG_ENTRY_QUANT = LAG_ENTRY_COPY + 1
 LAG_VALUE_MATMUL = LAG_ENTRY_QUANT + 1
-LAG_VALUE_COPY = LAG_VALUE_MATMUL + 1
-LAG_VALUE_TRANSPOSE = LAG_VALUE_COPY + 1
-LAG_VALUE_BIAS = LAG_VALUE_TRANSPOSE + 1
+LAG_VALUE_BIAS = LAG_VALUE_MATMUL + 1
 LAG_VALUE_QUANT = LAG_VALUE_BIAS + 1
 LAG_NORM_MATMUL = LAG_VALUE_QUANT + 1
 LAG_NORM_SUM = LAG_NORM_MATMUL + 1
@@ -129,6 +127,15 @@ def tile_advancedliquidneuralnetwork_pb_t_kernel(
             nc.sync.dma_start(out=vec_rows[SLICES * i : SLICES * (i + 1), :], in_=vec.rearrange("(m p) -> m p", p=P))
         nc.sync.dma_start(out=tau_rows[:], in_=tau.partition_broadcast(P))
 
+        wv_codes = const.tile([P, PACK, P], U32, align_bytes=64)
+        wv_scales = const.tile([P, PACK, P], U8, align_bytes=64)
+        nc.vector.tensor_copy(
+            out=wv_codes[:].bitcast(I32), in_=w_codes[:, W_V, :].bitcast(I32).rearrange("p (m j) -> p j m", j=PACK)
+        )
+        nc.vector.tensor_copy(
+            out=wv_scales[:].rearrange("p j m -> p m j"), in_=w_scales[:, W_V, :].rearrange("p (m j) -> p m j", j=PACK)
+        )
+
         ident = const.tile([P, P], F32)
         make_identity(nc, ident[:])
         ident_bf = const.tile([P, P], BF16)
@@ -216,23 +223,18 @@ def tile_advancedliquidneuralnetwork_pb_t_kernel(
 
         def value_matmul(t):
             if in_range(t):
-                v_ps = psum.tile([P, FEAT], F32, tag="bank")
-                mx_rows(v_ps, live["liq_mx", t][0], live["liq_mx", t][1], W_V)
-                live["v_ps", t] = v_ps
-
-        def value_copy(t):
-            if in_range(t):
-                v_planes = work.tile([P, PACK, P], F32, tag="v_planes")
-                nc.scalar.copy(
-                    out=v_planes[:].rearrange("r j p -> r p j"), in_=live["v_ps", t][:].rearrange("r (p j) -> r p j", j=PACK)
-                )
-                live["v_planes", t] = v_planes
-
-        def value_transposes(t):
-            if in_range(t):
+                liq_codes, liq_scales = live["liq_mx", t]
                 vt_ps = psum.tile([P, PACK, P], F32, tag="bank")
                 for j in range(PACK):
-                    nc.tensor.transpose(vt_ps[:, j, :], live["v_planes", t][:, j, :], ident[:])
+                    nc.tensor.matmul_mx(
+                        out=vt_ps[:, j, :],
+                        lhsT=wv_codes[:, j, :].bitcast(FP8X4),
+                        lhsT_scale=wv_scales[:, j, :],
+                        rhs=liq_codes[:].bitcast(FP8X4),
+                        rhs_scale=liq_scales[:],
+                        start=True,
+                        stop=True,
+                    )
                 live["vt_ps", t] = vt_ps
 
         def value_bias(t):
@@ -430,11 +432,9 @@ def tile_advancedliquidneuralnetwork_pb_t_kernel(
             norm_matmul(q - LAG_NORM_MATMUL)
             value_matmul(q - LAG_VALUE_MATMUL)
             gate_transposes(q - LAG_GATE_TRANSPOSE)
-            value_transposes(q - LAG_VALUE_TRANSPOSE)
             update_products(q - LAG_UPDATE_PRODUCT)
             entry_transposes(q)
             drive_copy(q - LAG_DRIVE_COPY)
-            value_copy(q - LAG_VALUE_COPY)
             norm_squares(q - LAG_NORM_SQUARES)
             norm_scale(q - LAG_NORM_SCALE)
             gate_tanh(q - LAG_GATE_TANH)

@@ -40,12 +40,13 @@ LAG_NORM_SCALE = LAG_NORM_INV_STD + 1
 LAG_GATE_TRANSPOSE = LAG_NORM_SCALE + TILES_PER_CHUNK
 LAG_GATE_SUM = LAG_GATE_TRANSPOSE + 1
 LAG_GATE_TANH = LAG_GATE_SUM + 1
-LAG_UPDATE_PRODUCT = LAG_GATE_TANH + SLICES
-LAG_UPDATE_SUM = LAG_UPDATE_PRODUCT + 1
+LAG_STATE_MIX = LAG_GATE_TANH + 1
+LAG_UPDATE_PRODUCT = LAG_STATE_MIX + SLICES
+LAG_UPDATE_COPY = LAG_UPDATE_PRODUCT + 1
 LAG_DRIVE_COPY = LAG_GATE_SUM - 2
 LAG_DRIVE_MATMUL = LAG_DRIVE_COPY - 1
 LAG_RESIDUAL = LAG_NORM_SUM - 1
-LAG_KEPT_STATE = LAG_UPDATE_SUM - 1
+LAG_STATE_TRANSPOSE = LAG_STATE_MIX - 1
 LOAD_AHEAD = 4
 CONSTANTS_ROUND = 8
 
@@ -112,7 +113,6 @@ def tile_advancedliquidneuralnetwork_pb_t_kernel(
 
         bv_words = const.tile([P, PACK], BF16)
         bo_rows = const.tile([P, FEAT], BF16)
-        tau_rows = const.tile([P, FEAT], BF16)
         vec_rows = const.tile([P, P], BF16)
         nc.vector.memset(vec_rows[:], 0.0)
 
@@ -125,7 +125,6 @@ def tile_advancedliquidneuralnetwork_pb_t_kernel(
         load_weight(W_IN, W_in_words, W_in_scales)
         for i, vec in enumerate((b_in, beta_att, g_att, tau)):
             nc.sync.dma_start(out=vec_rows[SLICES * i : SLICES * (i + 1), :], in_=vec.rearrange("(m p) -> m p", p=P))
-        nc.sync.dma_start(out=tau_rows[:], in_=tau.partition_broadcast(P))
 
         wv_codes = const.tile([P, PACK, P], U32, align_bytes=64)
         wv_scales = const.tile([P, PACK, P], U8, align_bytes=64)
@@ -148,18 +147,16 @@ def tile_advancedliquidneuralnetwork_pb_t_kernel(
         gain_col = vec_cols[:, 2 * SLICES : 3 * SLICES]
         rate_col = const.tile([P, SLICES], F32)
         rate_diag = const.tile([P, SLICES, P], F32)
-        keep_rows = const.tile([P, FEAT], F32)
+        pull_col = const.tile([P, SLICES], F32)
 
         def feature_constants():
             vec_ps = psum.tile([P, P], BF16, tag="bank")
             nc.tensor.transpose(vec_ps[:], vec_rows[:], ident_bf[:])
             nc.vector.tensor_copy(out=vec_cols[:], in_=vec_ps[:, 0 : 4 * SLICES])
-            nc.vector.tensor_scalar_add(out=keep_rows[:], in0=tau_rows[:], scalar1=TAU_EPS)
             nc.vector.tensor_add(out=shift_col[:], in0=vec_cols[:, 0:SLICES], in1=vec_cols[:, SLICES : 2 * SLICES])
-            nc.vector.reciprocal(out=keep_rows[:], in_=keep_rows[:])
             nc.vector.tensor_scalar_add(out=rate_col[:], in0=vec_cols[:, 3 * SLICES : 4 * SLICES], scalar1=TAU_EPS)
             nc.vector.tensor_scalar(
-                out=keep_rows[:], in0=keep_rows[:], scalar1=-1.0, scalar2=1.0, op0=ALU.mult, op1=ALU.add
+                out=pull_col[:], in0=vec_cols[:, 3 * SLICES : 4 * SLICES], scalar1=TAU_EPS, scalar2=-1.0, op0=ALU.add, op1=ALU.add
             )
             nc.vector.reciprocal(out=rate_col[:], in_=rate_col[:])
             for m in range(SLICES):
@@ -387,12 +384,25 @@ def tile_advancedliquidneuralnetwork_pb_t_kernel(
                 c, m = divmod(k, SLICES)
                 nc.scalar.activation(out=live["drive", c][:, m, :], in_=live["drive", c][:, m, :], func=ACT.Tanh)
 
-        def kept_state(t):
-            if in_range(t):
-                c, i = divmod(t, TILES_PER_CHUNK)
-                if i == 0:
-                    live["new_h", c] = work.tile([P, TILES_PER_CHUNK, FEAT], F32, tag="new_h", name="new_h")
-                nc.gpsimd.tensor_tensor(out=live["new_h", c][:, i, :], in0=live["h", c][:, i, :], in1=keep_rows[:], op=ALU.mult)
+        def state_transposes(k):
+            if in_range(k):
+                c, m = divmod(k, SLICES)
+                state_ps = psum.tile([P, TILES_PER_CHUNK, P], BF16, tag="bank")
+                for i in range(TILES_PER_CHUNK):
+                    nc.tensor.transpose(state_ps[:, i, :], live["h", c][:, i, m * P : (m + 1) * P], ident_bf[:])
+                live["state_ps", k] = state_ps
+
+        def state_mix(k):
+            if in_range(k):
+                c, m = divmod(k, SLICES)
+                nc.vector.scalar_tensor_tensor(
+                    out=live["drive", c][:, m, :],
+                    in0=live["state_ps", k][:].rearrange("p i r -> p (i r)"),
+                    scalar=pull_col[:, m : m + 1],
+                    in1=live["drive", c][:, m, :],
+                    op0=ALU.mult,
+                    op1=ALU.add,
+                )
 
         def update_products(t):
             if in_range(t):
@@ -408,44 +418,42 @@ def tile_advancedliquidneuralnetwork_pb_t_kernel(
                     )
                 live["pull_ps", t] = pull_ps
 
-        def update_sum(t):
+        def update_copy(t):
             if in_range(t):
                 c, i = divmod(t, TILES_PER_CHUNK)
-                nc.vector.tensor_tensor(
-                    out=live["new_h", c][:, i, :],
-                    in0=live["pull_ps", t][:].rearrange("r m f -> r (m f)"),
-                    in1=live["new_h", c][:, i, :],
-                    op=ALU.add,
-                )
+                if i == 0:
+                    live["new_h", c] = work.tile([P, TILES_PER_CHUNK, FEAT], F32, tag="new_h", name="new_h")
+                nc.scalar.copy(out=live["new_h", c][:, i, :], in_=live["pull_ps", t][:].rearrange("r m f -> r (m f)"))
                 if i == TILES_PER_CHUNK - 1:
                     nc.sync.dma_start(out=out_rows[:, chunk_rows(c), :], in_=live["new_h", c][:])
 
-        for q in range(ROW_TILES + LAG_UPDATE_SUM):
+        for q in range(ROW_TILES + LAG_UPDATE_COPY):
             c, i = divmod(q + LOAD_AHEAD, TILES_PER_CHUNK)
             if i == 0:
                 load_chunk("liq", liq_rows, c)
                 load_chunk("x", x_rows, c)
-                load_chunk("h", h_rows, c - LAG_KEPT_STATE // TILES_PER_CHUNK)
+                load_chunk("h", h_rows, c - LAG_STATE_TRANSPOSE // TILES_PER_CHUNK)
             if q == CONSTANTS_ROUND:
                 feature_constants()
             drive_matmul(q - LAG_DRIVE_MATMUL)
             norm_matmul(q - LAG_NORM_MATMUL)
             value_matmul(q - LAG_VALUE_MATMUL)
             gate_transposes(q - LAG_GATE_TRANSPOSE)
+            state_transposes(q - LAG_STATE_TRANSPOSE)
             update_products(q - LAG_UPDATE_PRODUCT)
             entry_transposes(q)
             drive_copy(q - LAG_DRIVE_COPY)
             norm_squares(q - LAG_NORM_SQUARES)
             norm_scale(q - LAG_NORM_SCALE)
             gate_tanh(q - LAG_GATE_TANH)
+            update_copy(q - LAG_UPDATE_COPY)
             entry_copy(q - LAG_ENTRY_COPY)
             norm_mean(q - LAG_NORM_MEAN)
             norm_inv_std(q - LAG_NORM_INV_STD)
-            kept_state(q - LAG_KEPT_STATE)
             norm_sum(q - LAG_NORM_SUM)
-            gate_sum(q - LAG_GATE_SUM)
             value_bias(q - LAG_VALUE_BIAS)
-            update_sum(q - LAG_UPDATE_SUM)
+            gate_sum(q - LAG_GATE_SUM)
+            state_mix(q - LAG_STATE_MIX)
             value_quantise(q - LAG_VALUE_QUANT)
             entry_quantise(q - LAG_ENTRY_QUANT)
             residual(q - LAG_RESIDUAL)

@@ -45,7 +45,7 @@ LAG_UPDATE_PRODUCT = LAG_STATE_MIX + SLICES
 LAG_UPDATE_COPY = LAG_UPDATE_PRODUCT + 1
 LAG_DRIVE_COPY = LAG_GATE_SUM - 2
 LAG_DRIVE_MATMUL = LAG_DRIVE_COPY - 1
-LAG_RESIDUAL = LAG_NORM_SUM - 1
+LAG_RESIDUAL = LAG_NORM_SUM - 2
 LAG_STATE_TRANSPOSE = LAG_STATE_MIX - 1
 LOAD_AHEAD = 4
 CONSTANTS_ROUND = 8
@@ -350,7 +350,7 @@ def tile_advancedliquidneuralnetwork_pb_t_kernel(
             if in_range(k):
                 c, m = divmod(k, SLICES)
                 if m == 0:
-                    live["drive", c] = work.tile([P, SLICES, CHUNK_ROWS], F32, tag="drive", name="drive")
+                    live["drive", c] = work.tile([P, SLICES, CHUNK_ROWS], F32, tag="drive", name="drive", bufs=4)
                 nc.scalar.activation(
                     out=live["drive", c][:, m, :],
                     in_=live["xin_ps", k][:],

@@ -33,9 +33,9 @@ LAG_VALUE_BIAS = LAG_VALUE_MATMUL + 1
 LAG_VALUE_QUANT = LAG_VALUE_BIAS + 1
 LAG_NORM_MATMUL = LAG_VALUE_QUANT + 1
 LAG_NORM_SUM = LAG_NORM_MATMUL + 1
-LAG_NORM_MEAN = LAG_NORM_SUM + 1
+LAG_NORM_MEAN = LAG_NORM_SUM
 LAG_NORM_SQUARES = LAG_NORM_MEAN + 1
-LAG_NORM_INV_STD = LAG_NORM_SQUARES + 1
+LAG_NORM_INV_STD = LAG_NORM_SQUARES
 LAG_NORM_SCALE = LAG_NORM_INV_STD + 1
 LAG_GATE_TRANSPOSE = LAG_NORM_SCALE + TILES_PER_CHUNK
 LAG_GATE_SUM = LAG_GATE_TRANSPOSE + 1
@@ -43,12 +43,12 @@ LAG_GATE_TANH = LAG_GATE_SUM + 1
 LAG_STATE_MIX = LAG_GATE_TANH + 1
 LAG_UPDATE_PRODUCT = LAG_STATE_MIX + SLICES
 LAG_UPDATE_COPY = LAG_UPDATE_PRODUCT + 1
-LAG_DRIVE_COPY = LAG_GATE_SUM - 2
-LAG_DRIVE_MATMUL = LAG_DRIVE_COPY - 1
+LAG_DRIVE_MATMUL = LAG_ENTRY_QUANT + TILES_PER_CHUNK
+LAG_DRIVE_COPY = LAG_DRIVE_MATMUL + 1
 LAG_RESIDUAL = LAG_NORM_SUM - 2
 LAG_STATE_TRANSPOSE = LAG_STATE_MIX - 1
 LOAD_AHEAD = 4
-CONSTANTS_ROUND = 8
+CONSTANTS_ROUND = 5
 
 FLOPS = 3 * 2 * ROWS * FEAT * FEAT
 
@@ -116,9 +116,13 @@ def tile_advancedliquidneuralnetwork_pb_t_kernel(
         vec_rows = const.tile([P, P], BF16)
         nc.vector.memset(vec_rows[:], 0.0)
 
-        load_chunk("liq", liq_rows, 0)
-        load_chunk("x", x_rows, 0)
-        load_weight(W_V, W_v_words, W_v_scales)
+        for name in ("liq", "x"):
+            live[name, 0] = loads.tile([P, TILES_PER_CHUNK, FEAT], BF16, tag=name, name=name, bufs=4 if name == "liq" else 3)
+        for i in range(TILES_PER_CHUNK):
+            nc.sync.dma_start(out=live["liq", 0][:, i : i + 1, :], in_=liq_rows[:, i : i + 1, :])
+            nc.sync.dma_start(out=live["x", 0][:, i : i + 1, :], in_=x_rows[:, i : i + 1, :])
+            if i == 0:
+                load_weight(W_V, W_v_words, W_v_scales)
         nc.sync.dma_start(out=bv_words[:], in_=b_v.rearrange("(p t) -> p t", t=PACK))
         load_weight(W_O, W_o_words, W_o_scales)
         nc.sync.dma_start(out=bo_rows[:], in_=b_o.partition_broadcast(P))
@@ -350,7 +354,7 @@ def tile_advancedliquidneuralnetwork_pb_t_kernel(
             if in_range(k):
                 c, m = divmod(k, SLICES)
                 if m == 0:
-                    live["drive", c] = work.tile([P, SLICES, CHUNK_ROWS], F32, tag="drive", name="drive", bufs=4)
+                    live["drive", c] = work.tile([P, SLICES, CHUNK_ROWS], F32, tag="drive", name="drive", bufs=6)
                 nc.scalar.activation(
                     out=live["drive", c][:, m, :],
                     in_=live["xin_ps", k][:],
@@ -424,8 +428,7 @@ def tile_advancedliquidneuralnetwork_pb_t_kernel(
                 if i == 0:
                     live["new_h", c] = work.tile([P, TILES_PER_CHUNK, FEAT], F32, tag="new_h", name="new_h")
                 nc.scalar.copy(out=live["new_h", c][:, i, :], in_=live["pull_ps", t][:].rearrange("r m f -> r (m f)"))
-                if i == TILES_PER_CHUNK - 1:
-                    nc.sync.dma_start(out=out_rows[:, chunk_rows(c), :], in_=live["new_h", c][:])
+                nc.sync.dma_start(out=out_rows[:, t : t + 1, :], in_=live["new_h", c][:, i : i + 1, :])
 
         for q in range(ROW_TILES + LAG_UPDATE_COPY):
             c, i = divmod(q + LOAD_AHEAD, TILES_PER_CHUNK)
@@ -442,15 +445,15 @@ def tile_advancedliquidneuralnetwork_pb_t_kernel(
             state_transposes(q - LAG_STATE_TRANSPOSE)
             update_products(q - LAG_UPDATE_PRODUCT)
             entry_transposes(q)
-            drive_copy(q - LAG_DRIVE_COPY)
             norm_squares(q - LAG_NORM_SQUARES)
+            drive_copy(q - LAG_DRIVE_COPY)
             norm_scale(q - LAG_NORM_SCALE)
             gate_tanh(q - LAG_GATE_TANH)
             update_copy(q - LAG_UPDATE_COPY)
             entry_copy(q - LAG_ENTRY_COPY)
+            norm_sum(q - LAG_NORM_SUM)
             norm_mean(q - LAG_NORM_MEAN)
             norm_inv_std(q - LAG_NORM_INV_STD)
-            norm_sum(q - LAG_NORM_SUM)
             value_bias(q - LAG_VALUE_BIAS)
             gate_sum(q - LAG_GATE_SUM)
             state_mix(q - LAG_STATE_MIX)

@@ -47,6 +47,7 @@ LAG_DRIVE_MATMUL = LAG_ENTRY_QUANT + TILES_PER_CHUNK
 LAG_DRIVE_COPY = LAG_DRIVE_MATMUL + 1
 LAG_RESIDUAL = LAG_NORM_SUM - 2
 LAG_STATE_TRANSPOSE = LAG_STATE_MIX - 1
+FIRST_PLAIN_CHUNK = 6
 LOAD_AHEAD = 4
 CONSTANTS_ROUND = 5
 
@@ -152,6 +153,7 @@ def tile_advancedliquidneuralnetwork_pb_t_kernel(
         rate_col = const.tile([P, SLICES], F32)
         rate_diag = const.tile([P, SLICES, P], F32)
         pull_col = const.tile([P, SLICES], F32)
+        keep_col = const.tile([P, SLICES], F32)
 
         def feature_constants():
             vec_ps = psum.tile([P, P], BF16, tag="bank")
@@ -165,6 +167,7 @@ def tile_advancedliquidneuralnetwork_pb_t_kernel(
             nc.vector.reciprocal(out=rate_col[:], in_=rate_col[:])
             for m in range(SLICES):
                 nc.vector.tensor_scalar_mul(out=rate_diag[:, m, :], in0=ident[:], scalar1=rate_col[:, m : m + 1])
+            nc.vector.tensor_scalar(out=keep_col[:], in0=rate_col[:], scalar1=-1.0, scalar2=1.0, op0=ALU.mult, op1=ALU.add)
 
         def in_range(t):
             return 0 <= t < ROW_TILES
@@ -396,13 +399,18 @@ def tile_advancedliquidneuralnetwork_pb_t_kernel(
                     nc.tensor.transpose(state_ps[:, i, :], live["h", c][:, i, m * P : (m + 1) * P], ident_bf[:])
                 live["state_ps", k] = state_ps
 
+        def gate_rate(k):
+            if in_range(k) and k // SLICES >= FIRST_PLAIN_CHUNK:
+                c, m = divmod(k, SLICES)
+                nc.vector.tensor_scalar_mul(out=live["drive", c][:, m, :], in0=live["drive", c][:, m, :], scalar1=rate_col[:, m : m + 1])
+
         def state_mix(k):
             if in_range(k):
                 c, m = divmod(k, SLICES)
                 nc.vector.scalar_tensor_tensor(
                     out=live["drive", c][:, m, :],
                     in0=live["state_ps", k][:].rearrange("p i r -> p (i r)"),
-                    scalar=pull_col[:, m : m + 1],
+                    scalar=(keep_col if c >= FIRST_PLAIN_CHUNK else pull_col)[:, m : m + 1],
                     in1=live["drive", c][:, m, :],
                     op0=ALU.mult,
                     op1=ALU.add,
@@ -413,13 +421,11 @@ def tile_advancedliquidneuralnetwork_pb_t_kernel(
                 c, i = divmod(t, TILES_PER_CHUNK)
                 pull_ps = psum.tile([P, SLICES, P], F32, tag="bank")
                 for m in range(SLICES):
-                    nc.tensor.matmul(
-                        out=pull_ps[:, m, :],
-                        lhsT=live["drive", c][:, m, i * P : (i + 1) * P],
-                        rhs=rate_diag[:, m, :],
-                        start=True,
-                        stop=True,
-                    )
+                    block = live["drive", c][:, m, i * P : (i + 1) * P]
+                    if c >= FIRST_PLAIN_CHUNK:
+                        nc.tensor.transpose(pull_ps[:, m, :], block, ident[:])
+                    else:
+                        nc.tensor.matmul(out=pull_ps[:, m, :], lhsT=block, rhs=rate_diag[:, m, :], start=True, stop=True)
                 live["pull_ps", t] = pull_ps
 
         def update_copy(t):
@@ -451,6 +457,7 @@ def tile_advancedliquidneuralnetwork_pb_t_kernel(
             gate_tanh(q - LAG_GATE_TANH)
             update_copy(q - LAG_UPDATE_COPY)
             entry_copy(q - LAG_ENTRY_COPY)
+            gate_rate(q - LAG_STATE_MIX)
             norm_sum(q - LAG_NORM_SUM)
             norm_mean(q - LAG_NORM_MEAN)
             norm_inv_std(q - LAG_NORM_INV_STD)

@@ -48,6 +48,8 @@ LAG_DRIVE_COPY = LAG_DRIVE_MATMUL + 1
 LAG_RESIDUAL = LAG_NORM_SUM - 2
 LAG_STATE_TRANSPOSE = LAG_STATE_MIX - 1
 FIRST_PLAIN_CHUNK = 6
+FIRST_CHUNK_BY_TILE = 6
+SAVED_BY_TILE = TILES_PER_CHUNK - 1
 LOAD_AHEAD = 4
 CONSTANTS_ROUND = 5
 
@@ -357,86 +359,107 @@ def tile_advancedliquidneuralnetwork_pb_t_kernel(
             if in_range(k):
                 c, m = divmod(k, SLICES)
                 if m == 0:
-                    live["drive", c] = work.tile([P, SLICES, CHUNK_ROWS], F32, tag="drive", name="drive", bufs=6)
+                    live["drive", c] = work.tile([P, TILES_PER_CHUNK, TILES_PER_CHUNK, P], F32, tag="drive", name="drive", bufs=6)
+                by_tile = c >= FIRST_CHUNK_BY_TILE
                 nc.scalar.activation(
-                    out=live["drive", c][:, m, :],
-                    in_=live["xin_ps", k][:],
+                    out=live["drive", c][:, :, m, :] if by_tile else live["drive", c][:, m, :, :],
+                    in_=live["xin_ps", k][:].rearrange("p (i r) -> p i r", r=P),
                     func=ACT.Identity,
                     bias=shift_col[:, m : m + 1],
                     scale=1.0,
                 )
 
-        def gate_transposes(k):
-            if in_range(k):
-                c, m = divmod(k, SLICES)
+        def mine(k, by_tile):
+            return in_range(k) and (k // TILES_PER_CHUNK >= FIRST_CHUNK_BY_TILE) == by_tile
+
+        def blocks(k, by_tile):
+            j = k % TILES_PER_CHUNK
+            return [(b, j, b) if by_tile else (b, b, j) for b in range(TILES_PER_CHUNK)]
+
+        def spans(k, by_tile):
+            if by_tile:
+                return [(m, slice(m * P, (m + 1) * P)) for m in range(SLICES)]
+            return [(k % TILES_PER_CHUNK, slice(0, CHUNK_ROWS))]
+
+        def unit_of(k):
+            c, j = divmod(k, TILES_PER_CHUNK)
+            return live["drive", c][:, j, :, :].rearrange("p b r -> p (b r)")
+
+        def gate_transposes(k, by_tile):
+            if mine(k, by_tile):
+                c = k // TILES_PER_CHUNK
                 normed_ps = psum.tile([P, TILES_PER_CHUNK, P], F32, tag="bank")
-                for i in range(TILES_PER_CHUNK):
-                    nc.tensor.transpose(normed_ps[:, i, :], live["u", c][:, i, m * P : (m + 1) * P], ident[:])
+                for b, i, m in blocks(k, by_tile):
+                    nc.tensor.transpose(normed_ps[:, b, :], live["u", c][:, i, m * P : (m + 1) * P], ident[:])
                 live["normed_ps", k] = normed_ps
 
-        def gate_sum(k):
-            if in_range(k):
-                c, m = divmod(k, SLICES)
-                nc.vector.scalar_tensor_tensor(
-                    out=live["drive", c][:, m, :],
-                    in0=live["normed_ps", k][:].rearrange("p i r -> p (i r)"),
-                    scalar=gain_col[:, m : m + 1],
-                    in1=live["drive", c][:, m, :],
-                    op0=ALU.mult,
-                    op1=ALU.add,
-                )
+        def gate_sum(k, by_tile):
+            if mine(k, by_tile):
+                c = k // TILES_PER_CHUNK
+                for m, cols in spans(k, by_tile):
+                    nc.vector.scalar_tensor_tensor(
+                        out=unit_of(k)[:, cols],
+                        in0=live["normed_ps", k][:].rearrange("p b r -> p (b r)")[:, cols],
+                        scalar=gain_col[:, m : m + 1],
+                        in1=unit_of(k)[:, cols],
+                        op0=ALU.mult,
+                        op1=ALU.add,
+                    )
 
-        def gate_tanh(k):
-            if in_range(k):
-                c, m = divmod(k, SLICES)
-                nc.scalar.activation(out=live["drive", c][:, m, :], in_=live["drive", c][:, m, :], func=ACT.Tanh)
+        def gate_tanh(k, by_tile):
+            if mine(k, by_tile):
+                nc.scalar.activation(out=unit_of(k), in_=unit_of(k), func=ACT.Tanh)
 
-        def state_transposes(k):
-            if in_range(k):
-                c, m = divmod(k, SLICES)
+        def state_transposes(k, by_tile):
+            if mine(k, by_tile):
+                c = k // TILES_PER_CHUNK
                 state_ps = psum.tile([P, TILES_PER_CHUNK, P], BF16, tag="bank")
-                for i in range(TILES_PER_CHUNK):
-                    nc.tensor.transpose(state_ps[:, i, :], live["h", c][:, i, m * P : (m + 1) * P], ident_bf[:])
+                for b, i, m in blocks(k, by_tile):
+                    nc.tensor.transpose(state_ps[:, b, :], live["h", c][:, i, m * P : (m + 1) * P], ident_bf[:])
                 live["state_ps", k] = state_ps
 
-        def gate_rate(k):
-            if in_range(k) and k // SLICES >= FIRST_PLAIN_CHUNK:
-                c, m = divmod(k, SLICES)
-                nc.vector.tensor_scalar_mul(out=live["drive", c][:, m, :], in0=live["drive", c][:, m, :], scalar1=rate_col[:, m : m + 1])
+        def gate_rate(k, by_tile):
+            if mine(k, by_tile) and k // TILES_PER_CHUNK >= FIRST_PLAIN_CHUNK:
+                c = k // TILES_PER_CHUNK
+                for m, cols in spans(k, by_tile):
+                    nc.vector.tensor_scalar_mul(out=unit_of(k)[:, cols], in0=unit_of(k)[:, cols], scalar1=rate_col[:, m : m + 1])
 
-        def state_mix(k):
-            if in_range(k):
-                c, m = divmod(k, SLICES)
-                nc.vector.scalar_tensor_tensor(
-                    out=live["drive", c][:, m, :],
-                    in0=live["state_ps", k][:].rearrange("p i r -> p (i r)"),
-                    scalar=(keep_col if c >= FIRST_PLAIN_CHUNK else pull_col)[:, m : m + 1],
-                    in1=live["drive", c][:, m, :],
-                    op0=ALU.mult,
-                    op1=ALU.add,
-                )
+        def state_mix(k, by_tile):
+            if mine(k, by_tile):
+                c = k // TILES_PER_CHUNK
+                for m, cols in spans(k, by_tile):
+                    nc.vector.scalar_tensor_tensor(
+                        out=unit_of(k)[:, cols],
+                        in0=live["state_ps", k][:].rearrange("p b r -> p (b r)")[:, cols],
+                        scalar=(keep_col if c >= FIRST_PLAIN_CHUNK else pull_col)[:, m : m + 1],
+                        in1=unit_of(k)[:, cols],
+                        op0=ALU.mult,
+                        op1=ALU.add,
+                    )
 
-        def update_products(t):
-            if in_range(t):
+        def update_products(t, by_tile):
+            if mine(t, by_tile):
                 c, i = divmod(t, TILES_PER_CHUNK)
                 pull_ps = psum.tile([P, SLICES, P], F32, tag="bank")
                 for m in range(SLICES):
-                    block = live["drive", c][:, m, i * P : (i + 1) * P]
+                    block = live["drive", c][:, i, m, :] if by_tile else live["drive", c][:, m, i, :]
                     if c >= FIRST_PLAIN_CHUNK:
                         nc.tensor.transpose(pull_ps[:, m, :], block, ident[:])
                     else:
                         nc.tensor.matmul(out=pull_ps[:, m, :], lhsT=block, rhs=rate_diag[:, m, :], start=True, stop=True)
                 live["pull_ps", t] = pull_ps
 
-        def update_copy(t):
-            if in_range(t):
+        def update_copy(t, by_tile):
+            if mine(t, by_tile):
                 c, i = divmod(t, TILES_PER_CHUNK)
                 if i == 0:
                     live["new_h", c] = work.tile([P, TILES_PER_CHUNK, FEAT], F32, tag="new_h", name="new_h")
                 nc.scalar.copy(out=live["new_h", c][:, i, :], in_=live["pull_ps", t][:].rearrange("r m f -> r (m f)"))
                 nc.sync.dma_start(out=out_rows[:, t : t + 1, :], in_=live["new_h", c][:, i : i + 1, :])
 
-        for q in range(ROW_TILES + LAG_UPDATE_COPY):
+        kinds = ((False, 0), (True, SAVED_BY_TILE))
+        last_round = max(FIRST_CHUNK_BY_TILE * TILES_PER_CHUNK - 1 + LAG_UPDATE_COPY, ROW_TILES - 1 + LAG_UPDATE_COPY - 2 * SAVED_BY_TILE)
+        for q in range(last_round + 1):
             c, i = divmod(q + LOAD_AHEAD, TILES_PER_CHUNK)
             if i == 0:
                 load_chunk("liq", liq_rows, c)
@@ -447,23 +470,31 @@ def tile_advancedliquidneuralnetwork_pb_t_kernel(
             drive_matmul(q - LAG_DRIVE_MATMUL)
             norm_matmul(q - LAG_NORM_MATMUL)
             value_matmul(q - LAG_VALUE_MATMUL)
-            gate_transposes(q - LAG_GATE_TRANSPOSE)
-            state_transposes(q - LAG_STATE_TRANSPOSE)
-            update_products(q - LAG_UPDATE_PRODUCT)
+            for by_tile, saved in kinds:
+                gate_transposes(q - LAG_GATE_TRANSPOSE + saved, by_tile)
+            for by_tile, saved in kinds:
+                state_transposes(q - LAG_STATE_TRANSPOSE + saved, by_tile)
+            for by_tile, saved in kinds:
+                update_products(q - LAG_UPDATE_PRODUCT + 2 * saved, by_tile)
             entry_transposes(q)
             norm_squares(q - LAG_NORM_SQUARES)
             drive_copy(q - LAG_DRIVE_COPY)
             norm_scale(q - LAG_NORM_SCALE)
-            gate_tanh(q - LAG_GATE_TANH)
-            update_copy(q - LAG_UPDATE_COPY)
+            for by_tile, saved in kinds:
+                gate_tanh(q - LAG_GATE_TANH + saved, by_tile)
+            for by_tile, saved in kinds:
+                update_copy(q - LAG_UPDATE_COPY + 2 * saved, by_tile)
             entry_copy(q - LAG_ENTRY_COPY)
-            gate_rate(q - LAG_STATE_MIX)
+            for by_tile, saved in kinds:
+                gate_rate(q - LAG_STATE_MIX + saved, by_tile)
             norm_sum(q - LAG_NORM_SUM)
             norm_mean(q - LAG_NORM_MEAN)
             norm_inv_std(q - LAG_NORM_INV_STD)
             value_bias(q - LAG_VALUE_BIAS)
-            gate_sum(q - LAG_GATE_SUM)
-            state_mix(q - LAG_STATE_MIX)
+            for by_tile, saved in kinds:
+                gate_sum(q - LAG_GATE_SUM + saved, by_tile)
+            for by_tile, saved in kinds:
+                state_mix(q - LAG_STATE_MIX + saved, by_tile)
             value_quantise(q - LAG_VALUE_QUANT)
             entry_quantise(q - LAG_ENTRY_QUANT)
             residual(q - LAG_RESIDUAL)

@@ -471,19 +471,19 @@ def tile_advancedliquidneuralnetwork_pb_t_kernel(
             norm_matmul(q - LAG_NORM_MATMUL)
             value_matmul(q - LAG_VALUE_MATMUL)
             for by_tile, saved in kinds:
+                update_products(q - LAG_UPDATE_PRODUCT + 2 * saved, by_tile)
+            for by_tile, saved in kinds:
                 gate_transposes(q - LAG_GATE_TRANSPOSE + saved, by_tile)
             for by_tile, saved in kinds:
                 state_transposes(q - LAG_STATE_TRANSPOSE + saved, by_tile)
-            for by_tile, saved in kinds:
-                update_products(q - LAG_UPDATE_PRODUCT + 2 * saved, by_tile)
             entry_transposes(q)
             norm_squares(q - LAG_NORM_SQUARES)
             drive_copy(q - LAG_DRIVE_COPY)
+            for by_tile, saved in kinds:
+                update_copy(q - LAG_UPDATE_COPY + 2 * saved, by_tile)
             norm_scale(q - LAG_NORM_SCALE)
             for by_tile, saved in kinds:
                 gate_tanh(q - LAG_GATE_TANH + saved, by_tile)
-            for by_tile, saved in kinds:
-                update_copy(q - LAG_UPDATE_COPY + 2 * saved, by_tile)
             entry_copy(q - LAG_ENTRY_COPY)
             for by_tile, saved in kinds:
                 gate_rate(q - LAG_STATE_MIX + saved, by_tile)

@@ -127,6 +127,8 @@ def tile_advancedliquidneuralnetwork_pb_t_kernel(
             if i == 0:
                 load_weight(W_V, W_v_words, W_v_scales)
         nc.sync.dma_start(out=bv_words[:], in_=b_v.rearrange("(p t) -> p t", t=PACK))
+        load_chunk("liq", liq_rows, 1)
+        load_chunk("x", x_rows, 1)
         load_weight(W_O, W_o_words, W_o_scales)
         nc.sync.dma_start(out=bo_rows[:], in_=b_o.partition_broadcast(P))
         load_weight(W_IN, W_in_words, W_in_scales)
@@ -135,12 +137,14 @@ def tile_advancedliquidneuralnetwork_pb_t_kernel(
 
         wv_codes = const.tile([P, PACK, P], U32, align_bytes=64)
         wv_scales = const.tile([P, PACK, P], U8, align_bytes=64)
-        nc.vector.tensor_copy(
-            out=wv_codes[:].bitcast(I32), in_=w_codes[:, W_V, :].bitcast(I32).rearrange("p (m j) -> p j m", j=PACK)
-        )
-        nc.vector.tensor_copy(
-            out=wv_scales[:].rearrange("p j m -> p m j"), in_=w_scales[:, W_V, :].rearrange("p (m j) -> p m j", j=PACK)
-        )
+
+        def order_value_weight():
+            nc.vector.tensor_copy(
+                out=wv_codes[:].bitcast(I32), in_=w_codes[:, W_V, :].bitcast(I32).rearrange("p (m j) -> p j m", j=PACK)
+            )
+            nc.vector.tensor_copy(
+                out=wv_scales[:].rearrange("p j m -> p m j"), in_=w_scales[:, W_V, :].rearrange("p (m j) -> p m j", j=PACK)
+            )
 
         ident = const.tile([P, P], F32)
         make_identity(nc, ident[:])
@@ -462,8 +466,9 @@ def tile_advancedliquidneuralnetwork_pb_t_kernel(
         for q in range(last_round + 1):
             c, i = divmod(q + LOAD_AHEAD, TILES_PER_CHUNK)
             if i == 0:
-                load_chunk("liq", liq_rows, c)
-                load_chunk("x", x_rows, c)
+                if c > 1:
+                    load_chunk("liq", liq_rows, c)
+                    load_chunk("x", x_rows, c)
                 load_chunk("h", h_rows, c - LAG_STATE_TRANSPOSE // TILES_PER_CHUNK)
             if q == CONSTANTS_ROUND:
                 feature_constants()
@@ -497,4 +502,6 @@ def tile_advancedliquidneuralnetwork_pb_t_kernel(
                 state_mix(q - LAG_STATE_MIX + saved, by_tile)
             value_quantise(q - LAG_VALUE_QUANT)
             entry_quantise(q - LAG_ENTRY_QUANT)
+            if q == LAG_ENTRY_QUANT:
+                order_value_weight()
             residual(q - LAG_RESIDUAL)

@@ -51,7 +51,7 @@ FIRST_PLAIN_CHUNK = 6
 FIRST_CHUNK_BY_TILE = 6
 SAVED_BY_TILE = TILES_PER_CHUNK - 1
 LOAD_AHEAD = 4
-CONSTANTS_ROUND = 5
+CONSTANTS_ROUND = 3
 
 FLOPS = 3 * 2 * ROWS * FEAT * FEAT
 
@@ -119,6 +119,10 @@ def tile_advancedliquidneuralnetwork_pb_t_kernel(
         vec_rows = const.tile([P, P], BF16)
         nc.vector.memset(vec_rows[:], 0.0)
 
+        nc.scalar.dma_start(out=bv_words[:], in_=b_v.rearrange("(p t) -> p t", t=PACK))
+        for i, vec in enumerate((b_in, beta_att, g_att, tau)):
+            nc.scalar.dma_start(out=vec_rows[SLICES * i : SLICES * (i + 1), :], in_=vec.rearrange("(m p) -> m p", p=P))
+
         for name in ("liq", "x"):
             live[name, 0] = loads.tile([P, TILES_PER_CHUNK, FEAT], BF16, tag=name, name=name, bufs=4 if name == "liq" else 3)
         for i in range(TILES_PER_CHUNK):
@@ -126,14 +130,11 @@ def tile_advancedliquidneuralnetwork_pb_t_kernel(
             nc.sync.dma_start(out=live["x", 0][:, i : i + 1, :], in_=x_rows[:, i : i + 1, :])
             if i == 0:
                 load_weight(W_V, W_v_words, W_v_scales)
-        nc.sync.dma_start(out=bv_words[:], in_=b_v.rearrange("(p t) -> p t", t=PACK))
         load_chunk("liq", liq_rows, 1)
         load_chunk("x", x_rows, 1)
         load_weight(W_O, W_o_words, W_o_scales)
         nc.sync.dma_start(out=bo_rows[:], in_=b_o.partition_broadcast(P))
         load_weight(W_IN, W_in_words, W_in_scales)
-        for i, vec in enumerate((b_in, beta_att, g_att, tau)):
-            nc.sync.dma_start(out=vec_rows[SLICES * i : SLICES * (i + 1), :], in_=vec.rearrange("(m p) -> m p", p=P))
 
         wv_codes = const.tile([P, PACK, P], U32, align_bytes=64)
         wv_scales = const.tile([P, PACK, P], U8, align_bytes=64)

@@ -161,6 +161,7 @@ def tile_advancedliquidneuralnetwork_pb_t_kernel(
         rate_diag = const.tile([P, SLICES, P], F32)
         pull_col = const.tile([P, SLICES], F32)
         keep_col = const.tile([P, SLICES], F32)
+        rate_rows = const.tile([P, FEAT], F32)
 
         def feature_constants():
             vec_ps = psum.tile([P, P], BF16, tag="bank")
@@ -175,6 +176,21 @@ def tile_advancedliquidneuralnetwork_pb_t_kernel(
             for m in range(SLICES):
                 nc.vector.tensor_scalar_mul(out=rate_diag[:, m, :], in0=ident[:], scalar1=rate_col[:, m : m + 1])
             nc.vector.tensor_scalar(out=keep_col[:], in0=rate_col[:], scalar1=-1.0, scalar2=1.0, op0=ALU.mult, op1=ALU.add)
+
+        def rate_broadcast_transposes():
+            rates_ps = psum.tile([P, SLICES, P], F32, tag="bank")
+            for m in range(SLICES):
+                nc.tensor.transpose(rates_ps[:, m, :], rate_col[:, m : m + 1].to_broadcast([P, P]), ident[:])
+            live["rates_ps", 0] = rates_ps
+
+        def rate_broadcast_copy():
+            nc.vector.tensor_copy(out=rate_rows[:], in_=live["rates_ps", 0][:].rearrange("p m f -> p (m f)"))
+
+        def by_vector(t):
+            return t // TILES_PER_CHUNK < FIRST_PLAIN_CHUNK and t % 4 == 1
+
+        def by_gpsimd(t):
+            return t % 2 == 1
 
         def in_range(t):
             return 0 <= t < ROW_TILES
@@ -270,12 +286,12 @@ def tile_advancedliquidneuralnetwork_pb_t_kernel(
                 )
                 live["v_mx", t] = (v_codes, v_scales)
 
-        def residual(t):
-            if in_range(t):
+        def residual(t, on_gpsimd):
+            if in_range(t) and by_gpsimd(t) == on_gpsimd:
                 c, i = divmod(t, TILES_PER_CHUNK)
-                if i == 0:
+                if ("u", c) not in live:
                     live["u", c] = work.tile([P, TILES_PER_CHUNK, FEAT], F32, tag="u", name="u", bufs=4)
-                nc.vector.tensor_tensor(out=live["u", c][:, i, :], in0=live["liq", c][:, i, :], in1=bo_rows[:], op=ALU.add)
+                (nc.gpsimd if on_gpsimd else nc.vector).tensor_tensor(out=live["u", c][:, i, :], in0=live["liq", c][:, i, :], in1=bo_rows[:], op=ALU.add)
 
         def norm_matmul(t):
             if in_range(t):
@@ -448,19 +464,22 @@ def tile_advancedliquidneuralnetwork_pb_t_kernel(
                 pull_ps = psum.tile([P, SLICES, P], F32, tag="bank")
                 for m in range(SLICES):
                     block = live["drive", c][:, i, m, :] if by_tile else live["drive", c][:, m, i, :]
-                    if c >= FIRST_PLAIN_CHUNK:
+                    if c >= FIRST_PLAIN_CHUNK or by_vector(t):
                         nc.tensor.transpose(pull_ps[:, m, :], block, ident[:])
                     else:
                         nc.tensor.matmul(out=pull_ps[:, m, :], lhsT=block, rhs=rate_diag[:, m, :], start=True, stop=True)
                 live["pull_ps", t] = pull_ps
 
-        def update_copy(t, by_tile):
-            if mine(t, by_tile):
-                c, i = divmod(t, TILES_PER_CHUNK)
-                if i == 0:
-                    live["new_h", c] = work.tile([P, TILES_PER_CHUNK, FEAT], F32, tag="new_h", name="new_h")
-                nc.scalar.copy(out=live["new_h", c][:, i, :], in_=live["pull_ps", t][:].rearrange("r m f -> r (m f)"))
-                nc.sync.dma_start(out=out_rows[:, t : t + 1, :], in_=live["new_h", c][:, i : i + 1, :])
+        def update_copy(t, by_tile, on_vector):
+            if mine(t, by_tile) and by_vector(t) == on_vector:
+                new_h = work.tile([P, 1, FEAT], F32, tag="new_h", name="new_h", bufs=6)
+                if on_vector:
+                    nc.vector.tensor_tensor(
+                        out=new_h[:, 0, :], in0=live["pull_ps", t][:].rearrange("r m f -> r (m f)"), in1=rate_rows[:], op=ALU.mult
+                    )
+                else:
+                    nc.scalar.copy(out=new_h[:, 0, :], in_=live["pull_ps", t][:].rearrange("r m f -> r (m f)"))
+                nc.sync.dma_start(out=out_rows[:, t : t + 1, :], in_=new_h[:])
 
         kinds = ((False, 0), (True, SAVED_BY_TILE))
         last_round = max(FIRST_CHUNK_BY_TILE * TILES_PER_CHUNK - 1 + LAG_UPDATE_COPY, ROW_TILES - 1 + LAG_UPDATE_COPY - 2 * SAVED_BY_TILE)
@@ -473,6 +492,8 @@ def tile_advancedliquidneuralnetwork_pb_t_kernel(
                 load_chunk("h", h_rows, c - LAG_STATE_TRANSPOSE // TILES_PER_CHUNK)
             if q == CONSTANTS_ROUND:
                 feature_constants()
+            if q == CONSTANTS_ROUND + 1:
+                rate_broadcast_transposes()
             drive_matmul(q - LAG_DRIVE_MATMUL)
             norm_matmul(q - LAG_NORM_MATMUL)
             value_matmul(q - LAG_VALUE_MATMUL)
@@ -486,7 +507,7 @@ def tile_advancedliquidneuralnetwork_pb_t_kernel(
             norm_squares(q - LAG_NORM_SQUARES)
             drive_copy(q - LAG_DRIVE_COPY)
             for by_tile, saved in kinds:
-                update_copy(q - LAG_UPDATE_COPY + 2 * saved, by_tile)
+                update_copy(q - LAG_UPDATE_COPY + 2 * saved, by_tile, False)
             norm_scale(q - LAG_NORM_SCALE)
             for by_tile, saved in kinds:
                 gate_tanh(q - LAG_GATE_TANH + saved, by_tile)
@@ -496,7 +517,10 @@ def tile_advancedliquidneuralnetwork_pb_t_kernel(
             norm_sum(q - LAG_NORM_SUM)
             norm_mean(q - LAG_NORM_MEAN)
             norm_inv_std(q - LAG_NORM_INV_STD)
+            residual(q - LAG_RESIDUAL, True)
             value_bias(q - LAG_VALUE_BIAS)
+            for by_tile, saved in kinds:
+                update_copy(q - LAG_UPDATE_COPY + 2 * saved, by_tile, True)
             for by_tile, saved in kinds:
                 gate_sum(q - LAG_GATE_SUM + saved, by_tile)
             for by_tile, saved in kinds:
@@ -505,4 +529,6 @@ def tile_advancedliquidneuralnetwork_pb_t_kernel(
             entry_quantise(q - LAG_ENTRY_QUANT)
             if q == LAG_ENTRY_QUANT:
                 order_value_weight()
-            residual(q - LAG_RESIDUAL)
+            residual(q - LAG_RESIDUAL, False)
+            if q == CONSTANTS_ROUND + 1:
+                rate_broadcast_copy()

from contextlib import ExitStack

import concourse.mybir as mybir
from concourse.masks import make_identity

F32 = mybir.dt.float32
BF16 = mybir.dt.bfloat16
I32 = mybir.dt.int32
U32 = mybir.dt.uint32
U8 = mybir.dt.uint8
FP8X4 = mybir.dt.float8_e4m3fn_x4
ALU = mybir.AluOpType
ACT = mybir.ActivationFunctionType

P = 128
PACK = 4
ROWS = 4096
FEAT = 512
ROW_TILES = ROWS // P
TILES_PER_CHUNK = 4
CHUNK_ROWS = TILES_PER_CHUNK * P
CHUNKS = ROW_TILES // TILES_PER_CHUNK
SLICES = FEAT // P
LN_EPS = 1e-5
TAU_EPS = 1e-6
W_IN, W_V, W_O = 0, 1, 2
LIQ, X = 0, 1

LAG_ENTRY_COPY = 1
LAG_ENTRY_QUANT = LAG_ENTRY_COPY + 1
LAG_VALUE_MATMUL = LAG_ENTRY_QUANT + 1
LAG_VALUE_BIAS = LAG_VALUE_MATMUL + 1
LAG_VALUE_QUANT = LAG_VALUE_BIAS + 1
LAG_NORM_MATMUL = LAG_VALUE_QUANT + 1
LAG_NORM_SUM = LAG_NORM_MATMUL + 1
LAG_NORM_MEAN = LAG_NORM_SUM
LAG_NORM_SQUARES = LAG_NORM_MEAN + 1
LAG_NORM_INV_STD = LAG_NORM_SQUARES
LAG_NORM_SCALE = LAG_NORM_INV_STD + 1
LAG_GATE_TRANSPOSE = LAG_NORM_SCALE + TILES_PER_CHUNK
LAG_GATE_SUM = LAG_GATE_TRANSPOSE + 1
LAG_GATE_TANH = LAG_GATE_SUM + 1
LAG_STATE_MIX = LAG_GATE_TANH + 1
LAG_UPDATE_PRODUCT = LAG_STATE_MIX + SLICES
LAG_UPDATE_COPY = LAG_UPDATE_PRODUCT + 1
LAG_DRIVE_MATMUL = LAG_ENTRY_QUANT + TILES_PER_CHUNK
LAG_DRIVE_COPY = LAG_DRIVE_MATMUL + 1
LAG_RESIDUAL = LAG_NORM_SUM - 2
LAG_STATE_TRANSPOSE = LAG_STATE_MIX - 1
FIRST_PLAIN_CHUNK = 6
FIRST_CHUNK_BY_TILE = 6
SAVED_BY_TILE = TILES_PER_CHUNK - 1
LOAD_AHEAD = 4
CONSTANTS_ROUND = 3

FLOPS = 3 * 2 * ROWS * FEAT * FEAT


def tile_advancedliquidneuralnetwork_pb_t_kernel(
    tc,
    liq,
    h,
    x,
    W_in_words,
    W_in_scales,
    b_in,
    W_v_words,
    W_v_scales,
    b_v,
    W_o_words,
    W_o_scales,
    b_o,
    g_att,
    beta_att,
    tau,
    out,
):
    nc = tc.nc

    liq_rows = liq.rearrange("(p i) f -> p i f", i=ROW_TILES)
    h_rows = h.rearrange("(p i) f -> p i f", i=ROW_TILES)
    x_rows = x.rearrange("(p i) f -> p i f", i=ROW_TILES)
    out_rows = out.rearrange("(p i) f -> p i f", i=ROW_TILES)

    with ExitStack() as stack:
        stack.enter_context(tc.manual_schedule())
        const = stack.enter_context(tc.tile_pool(name="const", bufs=1))
        loads = stack.enter_context(tc.tile_pool(name="loads", bufs=3))
        work = stack.enter_context(tc.tile_pool(name="work", bufs=3))
        psum = stack.enter_context(tc.psum_pool(name="psum", bufs=8))

        live = {}

        def chunk_rows(c):
            return slice(c * TILES_PER_CHUNK, (c + 1) * TILES_PER_CHUNK)

        def load_chunk(name, rows, c):
            if 0 <= c < CHUNKS:
                live[name, c] = loads.tile([P, TILES_PER_CHUNK, FEAT], BF16, tag=name, name=name, bufs=4 if name == "liq" else 3)
                nc.sync.dma_start(out=live[name, c][:], in_=rows[:, chunk_rows(c), :])

        w_codes = const.tile([P, 3, FEAT], U32, align_bytes=64)
        w_scales = const.tile([P, 3, FEAT], U8, align_bytes=64)
        nc.vector.memset(w_scales[:].bitcast(I32), 0)

        def load_weight(w, words, scales):
            nc.sync.dma_start(
                out=w_codes[:, w, :].bitcast(I32), in_=words.rearrange("g p n t -> (g p) (n t)").bitcast(I32)
            )
            scale_rows = scales.rearrange("g q n -> (g q) n").bitcast(I32)
            for quadrant in range(4):
                nc.sync.dma_start(
                    out=w_scales[32 * quadrant : 32 * quadrant + 4, w, :].bitcast(I32),
                    in_=scale_rows[4 * quadrant : 4 * quadrant + 4, :],
                )

        bv_words = const.tile([P, PACK], BF16)
        bo_rows = const.tile([P, FEAT], BF16)
        vec_rows = const.tile([P, P], BF16)
        nc.vector.memset(vec_rows[:], 0.0)

        nc.scalar.dma_start(out=bv_words[:], in_=b_v.rearrange("(p t) -> p t", t=PACK))
        for i, vec in enumerate((b_in, beta_att, g_att, tau)):
            nc.scalar.dma_start(out=vec_rows[SLICES * i : SLICES * (i + 1), :], in_=vec.rearrange("(m p) -> m p", p=P))

        for name in ("liq", "x"):
            live[name, 0] = loads.tile([P, TILES_PER_CHUNK, FEAT], BF16, tag=name, name=name, bufs=4 if name == "liq" else 3)
        for i in range(TILES_PER_CHUNK):
            nc.sync.dma_start(out=live["liq", 0][:, i : i + 1, :], in_=liq_rows[:, i : i + 1, :])
            nc.sync.dma_start(out=live["x", 0][:, i : i + 1, :], in_=x_rows[:, i : i + 1, :])
            if i == 0:
                load_weight(W_V, W_v_words, W_v_scales)
        load_chunk("liq", liq_rows, 1)
        load_chunk("x", x_rows, 1)
        load_weight(W_O, W_o_words, W_o_scales)
        nc.sync.dma_start(out=bo_rows[:], in_=b_o.partition_broadcast(P))
        load_weight(W_IN, W_in_words, W_in_scales)

        wv_codes = const.tile([P, PACK, P], U32, align_bytes=64)
        wv_scales = const.tile([P, PACK, P], U8, align_bytes=64)

        def order_value_weight():
            nc.vector.tensor_copy(
                out=wv_codes[:].bitcast(I32), in_=w_codes[:, W_V, :].bitcast(I32).rearrange("p (m j) -> p j m", j=PACK)
            )
            nc.vector.tensor_copy(
                out=wv_scales[:].rearrange("p j m -> p m j"), in_=w_scales[:, W_V, :].rearrange("p (m j) -> p m j", j=PACK)
            )

        ident = const.tile([P, P], F32)
        make_identity(nc, ident[:])
        ident_bf = const.tile([P, P], BF16)
        make_identity(nc, ident_bf[:])
        minus_half = const.tile([P, 1], F32)
        nc.vector.memset(minus_half[:], -0.5)

        vec_cols = const.tile([P, 4 * SLICES], F32)
        shift_col = const.tile([P, SLICES], F32)
        gain_col = vec_cols[:, 2 * SLICES : 3 * SLICES]
        rate_col = const.tile([P, SLICES], F32)
        rate_diag = const.tile([P, SLICES, P], F32)
        pull_col = const.tile([P, SLICES], F32)
        keep_col = const.tile([P, SLICES], F32)
        rate_rows = const.tile([P, FEAT], F32)

        def feature_constants():
            vec_ps = psum.tile([P, P], BF16, tag="bank")
            nc.tensor.transpose(vec_ps[:], vec_rows[:], ident_bf[:])
            nc.vector.tensor_copy(out=vec_cols[:], in_=vec_ps[:, 0 : 4 * SLICES])
            nc.vector.tensor_add(out=shift_col[:], in0=vec_cols[:, 0:SLICES], in1=vec_cols[:, SLICES : 2 * SLICES])
            nc.vector.tensor_scalar_add(out=rate_col[:], in0=vec_cols[:, 3 * SLICES : 4 * SLICES], scalar1=TAU_EPS)
            nc.vector.tensor_scalar(
                out=pull_col[:], in0=vec_cols[:, 3 * SLICES : 4 * SLICES], scalar1=TAU_EPS, scalar2=-1.0, op0=ALU.add, op1=ALU.add
            )
            nc.vector.reciprocal(out=rate_col[:], in_=rate_col[:])
            for m in range(SLICES):
                nc.vector.tensor_scalar_mul(out=rate_diag[:, m, :], in0=ident[:], scalar1=rate_col[:, m : m + 1])
            nc.vector.tensor_scalar(out=keep_col[:], in0=rate_col[:], scalar1=-1.0, scalar2=1.0, op0=ALU.mult, op1=ALU.add)

        def rate_broadcast_transposes():
            rates_ps = psum.tile([P, SLICES, P], F32, tag="bank")
            for m in range(SLICES):
                nc.tensor.transpose(rates_ps[:, m, :], rate_col[:, m : m + 1].to_broadcast([P, P]), ident[:])
            live["rates_ps", 0] = rates_ps

        def rate_broadcast_copy():
            nc.vector.tensor_copy(out=rate_rows[:], in_=live["rates_ps", 0][:].rearrange("p m f -> p (m f)"))

        def by_vector(t):
            return t // TILES_PER_CHUNK < FIRST_PLAIN_CHUNK and t % 4 == 1

        def by_gpsimd(t):
            return t % 2 == 1

        def in_range(t):
            return 0 <= t < ROW_TILES

        def mx_rows(acc, codes, scales, w):
            nc.tensor.matmul_mx(
                out=acc[:],
                lhsT=codes[:].bitcast(FP8X4),
                lhsT_scale=scales[:],
                rhs=w_codes[:, w, :].bitcast(FP8X4),
                rhs_scale=w_scales[:, w, :],
                start=True,
                stop=True,
            )

        def entry_transposes(t):
            if in_range(t):
                c, i = divmod(t, TILES_PER_CHUNK)
                planes = psum.tile([P, 2, 2, P], F32, tag="bank")
                for s, name in ((LIQ, "liq"), (X, "x")):
                    words = live[name, c][:, i, :].bitcast(F32)
                    for u in range(2):
                        nc.tensor.transpose(planes[:, s, u, :], words[:, u::2], ident[:])
                live["planes", t] = planes

        def entry_copy(t):
            if in_range(t):
                grouped = work.tile([P, 2, P, PACK], BF16, tag="in_grouped", align_bytes=64)
                grouped_words = (
                    grouped[:].rearrange("p s r t -> p (s r t)").bitcast(F32).rearrange("p (s r u) -> p s r u", r=P, u=2)
                )
                nc.scalar.copy(out=grouped_words, in_=live["planes", t][:].rearrange("p s u r -> p s r u"))
                live["in_grouped", t] = grouped

        def entry_quantise(t):
            if in_range(t):
                c, i = divmod(t, TILES_PER_CHUNK)
                grouped = live["in_grouped", t]
                liq_codes = work.tile([P, P], U32, tag="liq_codes", align_bytes=64)
                liq_scales = work.tile([P, P], U8, tag="liq_scales", align_bytes=64)
                nc.vector.quantize_mx(
                    out=liq_codes[:].bitcast(FP8X4),
                    scales=liq_scales[:],
                    in_=grouped[:, LIQ, :, :].rearrange("p r t -> p (r t)"),
                )
                live["liq_mx", t] = (liq_codes, liq_scales)
                if i == 0:
                    x_codes = work.tile([P, CHUNK_ROWS], U32, tag="x_codes", align_bytes=64, bufs=5)
                    x_scales = work.tile([P, CHUNK_ROWS], U8, tag="x_scales", align_bytes=64, bufs=5)
                    live["x_mx", c] = (x_codes, x_scales)
                x_codes, x_scales = live["x_mx", c]
                nc.vector.quantize_mx(
                    out=x_codes[:, i * P : (i + 1) * P].bitcast(FP8X4),
                    scales=x_scales[:, i * P : (i + 1) * P],
                    in_=grouped[:, X, :, :].rearrange("p r t -> p (r t)"),
                )

        def value_matmul(t):
            if in_range(t):
                liq_codes, liq_scales = live["liq_mx", t]
                vt_ps = psum.tile([P, PACK, P], F32, tag="bank")
                for j in range(PACK):
                    nc.tensor.matmul_mx(
                        out=vt_ps[:, j, :],
                        lhsT=wv_codes[:, j, :].bitcast(FP8X4),
                        lhsT_scale=wv_scales[:, j, :],
                        rhs=liq_codes[:].bitcast(FP8X4),
                        rhs_scale=liq_scales[:],
                        start=True,
                        stop=True,
                    )
                live["vt_ps", t] = vt_ps

        def value_bias(t):
            if in_range(t):
                grouped = work.tile([P, P, PACK], BF16, tag="v_grouped", align_bytes=64)
                nc.vector.tensor_tensor(
                    out=grouped[:],
                    in0=live["vt_ps", t][:].rearrange("p j r -> p r j"),
                    in1=bv_words[:].unsqueeze(1).to_broadcast([P, P, PACK]),
                    op=ALU.add,
                )
                live["v_grouped", t] = grouped

        def value_quantise(t):
            if in_range(t):
                v_codes = work.tile([P, P], U32, tag="v_codes", align_bytes=64)
                v_scales = work.tile([P, P], U8, tag="v_scales", align_bytes=64)
                nc.vector.quantize_mx(
                    out=v_codes[:].bitcast(FP8X4),
                    scales=v_scales[:],
                    in_=live["v_grouped", t][:].rearrange("p r j -> p (r j)"),
                )
                live["v_mx", t] = (v_codes, v_scales)

        def residual(t, on_gpsimd):
            if in_range(t) and by_gpsimd(t) == on_gpsimd:
                c, i = divmod(t, TILES_PER_CHUNK)
                if ("u", c) not in live:
                    live["u", c] = work.tile([P, TILES_PER_CHUNK, FEAT], F32, tag="u", name="u", bufs=4)
                (nc.gpsimd if on_gpsimd else nc.vector).tensor_tensor(out=live["u", c][:, i, :], in0=live["liq", c][:, i, :], in1=bo_rows[:], op=ALU.add)

        def norm_matmul(t):
            if in_range(t):
                att_ps = psum.tile([P, FEAT], F32, tag="bank")
                mx_rows(att_ps, live["v_mx", t][0], live["v_mx", t][1], W_O)
                live["att_ps", t] = att_ps

        def norm_sum(t):
            if in_range(t):
                c, i = divmod(t, TILES_PER_CHUNK)
                row_sum = work.tile([P, 1], F32, tag="row_sum")
                nc.vector.scalar_tensor_tensor(
                    out=live["u", c][:, i, :],
                    in0=live["att_ps", t][:],
                    scalar=1.0,
                    in1=live["u", c][:, i, :],
                    op0=ALU.mult,
                    op1=ALU.add,
                    accum_out=row_sum[:],
                )
                live["row_sum", t] = row_sum

        def norm_mean(t):
            if in_range(t):
                minus_mean = work.tile([P, 1], F32, tag="minus_mean", bufs=4)
                nc.gpsimd.tensor_scalar(
                    out=minus_mean[:], in0=live["row_sum", t][:], scalar1=-1.0 / FEAT, scalar2=0.0, op0=ALU.mult, op1=ALU.add
                )
                live["minus_mean", t] = minus_mean

        def norm_squares(t):
            if in_range(t):
                c, i = divmod(t, TILES_PER_CHUNK)
                squares = work.tile([P, FEAT], BF16, tag="squares")
                square_sum = work.tile([P, 1], F32, tag="square_sum")
                nc.scalar.activation(
                    out=squares[:],
                    in_=live["u", c][:, i, :],
                    func=ACT.Square,
                    bias=live["minus_mean", t][:],
                    scale=1.0,
                    accum_out=square_sum[:],
                )
                live["square_sum", t] = square_sum

        def norm_inv_std(t):
            if in_range(t):
                inv_std = work.tile([P, 1], F32, tag="inv_std")
                offset = work.tile([P, 1], F32, tag="offset")
                nc.gpsimd.tensor_scalar(
                    out=inv_std[:], in0=live["square_sum", t][:], scalar1=1.0 / FEAT, scalar2=LN_EPS, op0=ALU.mult, op1=ALU.add
                )
                nc.gpsimd.tensor_tensor(out=inv_std[:], in0=inv_std[:], in1=minus_half[:], op=ALU.pow)
                nc.gpsimd.tensor_tensor(out=offset[:], in0=live["minus_mean", t][:], in1=inv_std[:], op=ALU.mult)
                live["inv_std", t] = inv_std
                live["offset", t] = offset

        def norm_scale(t):
            if in_range(t):
                c, i = divmod(t, TILES_PER_CHUNK)
                nc.scalar.activation(
                    out=live["u", c][:, i, :],
                    in_=live["u", c][:, i, :],
                    func=ACT.Identity,
                    bias=live["offset", t][:],
                    scale=live["inv_std", t][:],
                )

        def drive_matmul(k):
            if in_range(k):
                c, m = divmod(k, SLICES)
                x_codes, x_scales = live["x_mx", c]
                xin_ps = psum.tile([P, CHUNK_ROWS], F32, tag="bank")
                nc.tensor.matmul_mx(
                    out=xin_ps[:],
                    lhsT=w_codes[:, W_IN, m * P : (m + 1) * P].bitcast(FP8X4),
                    lhsT_scale=w_scales[:, W_IN, m * P : (m + 1) * P],
                    rhs=x_codes[:].bitcast(FP8X4),
                    rhs_scale=x_scales[:],
                    start=True,
                    stop=True,
                )
                live["xin_ps", k] = xin_ps

        def drive_copy(k):
            if in_range(k):
                c, m = divmod(k, SLICES)
                if m == 0:
                    live["drive", c] = work.tile([P, TILES_PER_CHUNK, TILES_PER_CHUNK, P], F32, tag="drive", name="drive", bufs=6)
                by_tile = c >= FIRST_CHUNK_BY_TILE
                nc.scalar.activation(
                    out=live["drive", c][:, :, m, :] if by_tile else live["drive", c][:, m, :, :],
                    in_=live["xin_ps", k][:].rearrange("p (i r) -> p i r", r=P),
                    func=ACT.Identity,
                    bias=shift_col[:, m : m + 1],
                    scale=1.0,
                )

        def mine(k, by_tile):
            return in_range(k) and (k // TILES_PER_CHUNK >= FIRST_CHUNK_BY_TILE) == by_tile

        def blocks(k, by_tile):
            j = k % TILES_PER_CHUNK
            return [(b, j, b) if by_tile else (b, b, j) for b in range(TILES_PER_CHUNK)]

        def spans(k, by_tile):
            if by_tile:
                return [(m, slice(m * P, (m + 1) * P)) for m in range(SLICES)]
            return [(k % TILES_PER_CHUNK, slice(0, CHUNK_ROWS))]

        def unit_of(k):
            c, j = divmod(k, TILES_PER_CHUNK)
            return live["drive", c][:, j, :, :].rearrange("p b r -> p (b r)")

        def gate_transposes(k, by_tile):
            if mine(k, by_tile):
                c = k // TILES_PER_CHUNK
                normed_ps = psum.tile([P, TILES_PER_CHUNK, P], F32, tag="bank")
                for b, i, m in blocks(k, by_tile):
                    nc.tensor.transpose(normed_ps[:, b, :], live["u", c][:, i, m * P : (m + 1) * P], ident[:])
                live["normed_ps", k] = normed_ps

        def gate_sum(k, by_tile):
            if mine(k, by_tile):
                c = k // TILES_PER_CHUNK
                for m, cols in spans(k, by_tile):
                    nc.vector.scalar_tensor_tensor(
                        out=unit_of(k)[:, cols],
                        in0=live["normed_ps", k][:].rearrange("p b r -> p (b r)")[:, cols],
                        scalar=gain_col[:, m : m + 1],
                        in1=unit_of(k)[:, cols],
                        op0=ALU.mult,
                        op1=ALU.add,
                    )

        def gate_tanh(k, by_tile):
            if mine(k, by_tile):
                nc.scalar.activation(out=unit_of(k), in_=unit_of(k), func=ACT.Tanh)

        def state_transposes(k, by_tile):
            if mine(k, by_tile):
                c = k // TILES_PER_CHUNK
                state_ps = psum.tile([P, TILES_PER_CHUNK, P], BF16, tag="bank")
                for b, i, m in blocks(k, by_tile):
                    nc.tensor.transpose(state_ps[:, b, :], live["h", c][:, i, m * P : (m + 1) * P], ident_bf[:])
                live["state_ps", k] = state_ps

        def gate_rate(k, by_tile):
            if mine(k, by_tile) and k // TILES_PER_CHUNK >= FIRST_PLAIN_CHUNK:
                c = k // TILES_PER_CHUNK
                for m, cols in spans(k, by_tile):
                    nc.vector.tensor_scalar_mul(out=unit_of(k)[:, cols], in0=unit_of(k)[:, cols], scalar1=rate_col[:, m : m + 1])

        def state_mix(k, by_tile):
            if mine(k, by_tile):
                c = k // TILES_PER_CHUNK
                for m, cols in spans(k, by_tile):
                    nc.vector.scalar_tensor_tensor(
                        out=unit_of(k)[:, cols],
                        in0=live["state_ps", k][:].rearrange("p b r -> p (b r)")[:, cols],
                        scalar=(keep_col if c >= FIRST_PLAIN_CHUNK else pull_col)[:, m : m + 1],
                        in1=unit_of(k)[:, cols],
                        op0=ALU.mult,
                        op1=ALU.add,
                    )

        def update_products(t, by_tile):
            if mine(t, by_tile):
                c, i = divmod(t, TILES_PER_CHUNK)
                pull_ps = psum.tile([P, SLICES, P], F32, tag="bank")
                for m in range(SLICES):
                    block = live["drive", c][:, i, m, :] if by_tile else live["drive", c][:, m, i, :]
                    if c >= FIRST_PLAIN_CHUNK or by_vector(t):
                        nc.tensor.transpose(pull_ps[:, m, :], block, ident[:])
                    else:
                        nc.tensor.matmul(out=pull_ps[:, m, :], lhsT=block, rhs=rate_diag[:, m, :], start=True, stop=True)
                live["pull_ps", t] = pull_ps

        def update_copy(t, by_tile, on_vector):
            if mine(t, by_tile) and by_vector(t) == on_vector:
                new_h = work.tile([P, 1, FEAT], F32, tag="new_h", name="new_h", bufs=6)
                if on_vector:
                    nc.vector.tensor_tensor(
                        out=new_h[:, 0, :], in0=live["pull_ps", t][:].rearrange("r m f -> r (m f)"), in1=rate_rows[:], op=ALU.mult
                    )
                else:
                    nc.scalar.copy(out=new_h[:, 0, :], in_=live["pull_ps", t][:].rearrange("r m f -> r (m f)"))
                nc.sync.dma_start(out=out_rows[:, t : t + 1, :], in_=new_h[:])

        kinds = ((False, 0), (True, SAVED_BY_TILE))
        last_round = max(FIRST_CHUNK_BY_TILE * TILES_PER_CHUNK - 1 + LAG_UPDATE_COPY, ROW_TILES - 1 + LAG_UPDATE_COPY - 2 * SAVED_BY_TILE)
        for q in range(last_round + 1):
            c, i = divmod(q + LOAD_AHEAD, TILES_PER_CHUNK)
            if i == 0:
                if c > 1:
                    load_chunk("liq", liq_rows, c)
                    load_chunk("x", x_rows, c)
                load_chunk("h", h_rows, c - LAG_STATE_TRANSPOSE // TILES_PER_CHUNK)
            if q == CONSTANTS_ROUND:
                feature_constants()
            if q == CONSTANTS_ROUND + 1:
                rate_broadcast_transposes()
            drive_matmul(q - LAG_DRIVE_MATMUL)
            norm_matmul(q - LAG_NORM_MATMUL)
            value_matmul(q - LAG_VALUE_MATMUL)
            for by_tile, saved in kinds:
                update_products(q - LAG_UPDATE_PRODUCT + 2 * saved, by_tile)
            for by_tile, saved in kinds:
                gate_transposes(q - LAG_GATE_TRANSPOSE + saved, by_tile)
            for by_tile, saved in kinds:
                state_transposes(q - LAG_STATE_TRANSPOSE + saved, by_tile)
            entry_transposes(q)
            norm_squares(q - LAG_NORM_SQUARES)
            drive_copy(q - LAG_DRIVE_COPY)
            for by_tile, saved in kinds:
                update_copy(q - LAG_UPDATE_COPY + 2 * saved, by_tile, False)
            norm_scale(q - LAG_NORM_SCALE)
            for by_tile, saved in kinds:
                gate_tanh(q - LAG_GATE_TANH + saved, by_tile)
            entry_copy(q - LAG_ENTRY_COPY)
            for by_tile, saved in kinds:
                gate_rate(q - LAG_STATE_MIX + saved, by_tile)
            norm_sum(q - LAG_NORM_SUM)
            norm_mean(q - LAG_NORM_MEAN)
            norm_inv_std(q - LAG_NORM_INV_STD)
            residual(q - LAG_RESIDUAL, True)
            value_bias(q - LAG_VALUE_BIAS)
            for by_tile, saved in kinds:
                update_copy(q - LAG_UPDATE_COPY + 2 * saved, by_tile, True)
            for by_tile, saved in kinds:
                gate_sum(q - LAG_GATE_SUM + saved, by_tile)
            for by_tile, saved in kinds:
                state_mix(q - LAG_STATE_MIX + saved, by_tile)
            value_quantise(q - LAG_VALUE_QUANT)
            entry_quantise(q - LAG_ENTRY_QUANT)
            if q == LAG_ENTRY_QUANT:
                order_value_weight()
            residual(q - LAG_RESIDUAL, False)
            if q == CONSTANTS_ROUND + 1:
                rate_broadcast_copy()
